import numpy as np
import ml_dtypes


def mxq(x, axis, fmt="e4m3"):
    dtype, down = {"e4m3": (ml_dtypes.float8_e4m3fn, 7), "e5m2": (ml_dtypes.float8_e5m2, 14)}[fmt]
    v = np.moveaxis(np.asarray(x, np.float32).astype(ml_dtypes.bfloat16).astype(np.float64), axis, -1)
    blocks = v.reshape(v.shape[:-1] + (-1, 32))
    amax = np.abs(blocks).max(-1, keepdims=True)
    byte = np.maximum(np.where(amax > 0, np.frexp(amax)[1] - 1 + 127, 0) - down, 1)
    scale = np.exp2(byte - 127.0)
    codes = (blocks / scale).astype(np.float32).astype(dtype).astype(np.float64)
    return np.moveaxis((codes * scale).reshape(v.shape), -1, axis)


WIDE = False


def mx_kscale(k):
    if not WIDE:
        return np.ones(k)
    levels = np.array([10, -10, 5, -5, 0])
    if k % 512:
        return np.exp2(np.random.permutation(np.resize(levels, k // 32))).repeat(32)
    a = np.empty((k // 512, 16))
    for p in range(k // 512):
        a[p, :8] = np.random.permutation(np.resize(levels, 8))
        for g in range(8):
            far = levels[np.abs(levels - a[p, g]) >= 10]
            a[p, g + 8] = far[np.random.randint(len(far))]
    return np.exp2(a.ravel()).repeat(32)


BF16 = ml_dtypes.bfloat16


def bf(x):
    return np.asarray(x, np.float32).astype(BF16)


def f64(x):
    return np.asarray(x).astype(np.float64)


B, STOCH, ACT_DIM, HIDDEN, DETER = 256, 1024, 512, 2048, 2048
EPS = 1e-4
DT_MIN = 1e-4


def softplus(v):
    return np.maximum(v, 0.0) + np.log1p(np.exp(-np.abs(v)))


def sigmoid(v):
    return 1.0 / (1.0 + np.exp(-v))


def rmsnorm(v, w):
    return v * (1.0 / np.sqrt(np.mean(v * v, axis=-1, keepdims=True) + EPS)) * w


def setup_inputs():
    s = mx_kscale(DETER)
    r = np.maximum(s, 1.0)

    def w():
        return np.random.standard_normal((DETER, DETER)) / np.sqrt(DETER) / s

    def bias():
        return np.random.standard_normal(DETER) * 0.2

    return {"x": bf(np.random.standard_normal((B, DETER)) * 0.9 * s),
            "deter": bf(np.random.standard_normal((B, DETER))),
            "a_base": bf(np.random.standard_normal(DETER)),
            "dt_w": bf(w()), "dt_b": bf(bias()),
            "b_w": bf(w()), "b_b": bf(bias()),
            "c_w": bf(w() / r[:, None]), "c_b": bf(bias() / r),
            "z_w": bf(w()), "z_b": bf(bias()),
            "skip": bf(np.random.standard_normal(DETER) * 0.5 / s),
            "norm_w": bf(1.0 + 0.1 * np.random.standard_normal(DETER))}


def reference(x, deter, a_base, dt_w, dt_b, b_w, b_b, c_w, c_b, z_w, z_b, skip, norm_w):
    x, deter = f64(x), f64(deter)
    xq = mxq(x, 1, "e4m3")
    dt = softplus((xq @ mxq(f64(dt_w), 1, "e4m3").T) + f64(dt_b)) + DT_MIN
    a = -softplus(f64(a_base))
    b = np.tanh((xq @ mxq(f64(b_w), 1, "e4m3").T) + f64(b_b))
    c = (xq @ mxq(f64(c_w), 1, "e4m3").T) + f64(c_b)
    z = sigmoid((xq @ mxq(f64(z_w), 1, "e4m3").T) + f64(z_b))
    state = np.exp(a * dt) * deter + dt * b * x
    y = c * state + f64(skip) * x
    out = z * y + (1.0 - z) * deter
    return rmsnorm(out, f64(norm_w))

@@ -1,0 +1,542 @@
+from contextlib import ExitStack
+
+import concourse.mybir as mybir
+from concourse.masks import make_identity
+
+F32 = mybir.dt.float32
+BF16 = mybir.dt.bfloat16
+U32 = mybir.dt.uint32
+U8 = mybir.dt.uint8
+FP8X4 = mybir.dt.float8_e4m3fn_x4
+ACT = mybir.ActivationFunctionType
+ALU = mybir.AluOpType
+
+P = 128
+TOKENS = 256
+CHANNELS = 2048
+PAIR = 2
+PACK = 4
+PASSES = CHANNELS // (P * PACK)
+GROUP_ROWS = PAIR * P
+GROUPS = CHANNELS // GROUP_ROWS
+GROUP_COLS = PAIR * TOKENS
+ROW_WORDS = CHANNELS // PAIR
+BANK = 512
+BANKS_PER_ROW = ROW_WORDS // BANK
+BANKS_PER_GROUP = PAIR * BANKS_PER_ROW
+
+GATES = ["dt", "c", "b", "z"]
+VECTOR_HELP_GROUPS = 20
+MULTIPLY_LAG = 2
+ONES_COLS = 32
+FLIP_BANKS = 5
+SUM_BANKS = 2
+LATE_BANKS = 1
+LOADS_AHEAD = 3
+EPS = 1e-4
+DT_MIN = 1e-4
+EXP_CAP = 20.0
+
+A_BASE = 0
+DT_B = 1
+B_B = 2
+C_B = 3
+Z_B = 4
+SKIP = 5
+NORM_W = 6
+
+FLOPS = 4 * 2 * TOKENS * CHANNELS * CHANNELS
+
+
+def tile_mamba2backbone_pb_kernel(
+    tc, x, deter, a_base, dt_w, dt_b, b_w, b_b, c_w, c_b, z_w, z_b, skip, norm_w, out
+):
+    nc = tc.nc
+    weights = {"dt": dt_w, "c": c_w, "b": b_w, "z": z_w}
+    vectors = [a_base, dt_b, b_b, c_b, z_b, skip, norm_w]
+
+    with ExitStack() as stack:
+        const = stack.enter_context(tc.tile_pool(name="const", bufs=1))
+        keep = stack.enter_context(tc.tile_pool(name="keep", bufs=1))
+        raw_pool = stack.enter_context(tc.tile_pool(name="raw", bufs=LOADS_AHEAD + 2))
+        grouped_pool = stack.enter_context(tc.tile_pool(name="grouped", bufs=3))
+        mx_pool = stack.enter_context(tc.tile_pool(name="mx", bufs=2))
+        temp = stack.enter_context(tc.tile_pool(name="temp", bufs=3))
+        store_pool = stack.enter_context(tc.tile_pool(name="store", bufs=4))
+        flip_psum = stack.enter_context(tc.psum_pool(name="flip", bufs=FLIP_BANKS))
+        sum_psum = stack.enter_context(tc.psum_pool(name="sums", bufs=SUM_BANKS))
+        late_psum = stack.enter_context(tc.psum_pool(name="late", bufs=LATE_BANKS))
+        stack.enter_context(tc.manual_schedule())
+
+        ident = const.tile([P, P], F32)
+        make_identity(nc, ident[:])
+        one_col = const.tile([P, 1], F32)
+        nc.vector.memset(one_col[:], 1.0)
+        eps_col = const.tile([P, 1], F32)
+        nc.vector.memset(eps_col[:], EPS)
+        sqrt_warm = const.tile([P, 1], F32)
+        ones = const.tile([P, ONES_COLS], F32)
+        nc.vector.memset(ones[:], 1.0)
+
+        def load_rows(rows_view):
+            rows = raw_pool.tile([P, PAIR * CHANNELS], BF16, tag="raw")
+            nc.sync.dma_start(out=rows[:].rearrange("p (r k) -> p r k", r=PAIR), in_=rows_view)
+            return rows
+
+        raw = {}
+
+        def load_group(index):
+            gate, j = GATES[index // GROUPS], index % GROUPS
+            g, u = j // PAIR, j % PAIR
+            rows = weights[gate][P * PACK * g : P * PACK * (g + 1), :]
+            rows = rows.rearrange("(p c) k -> p c k", c=PACK)
+            raw[index] = load_rows(rows[:, PAIR * u : PAIR * (u + 1), :])
+
+        load_group(0)
+        x_rows = load_rows(x.rearrange("(t p) k -> p t k", p=P))
+        vector_rows = const.tile([P, PACK * P], BF16)
+        nc.vector.memset(vector_rows[:], 0.0)
+        for i, vector in enumerate(vectors):
+            nc.scalar.dma_start(
+                out=vector_rows[PASSES * i : PASSES * (i + 1), :],
+                in_=vector.rearrange("(g c) -> g c", g=PASSES),
+            )
+        load_group(1)
+        load_group(2)
+        deter_rows = load_rows(deter.rearrange("(t p) k -> p t k", p=P))
+
+        def empty_bank(on_vector, out_words, bank_view):
+            if on_vector:
+                nc.vector.tensor_copy(out=out_words, in_=bank_view)
+            else:
+                nc.scalar.copy(out=out_words, in_=bank_view)
+
+        def transpose_tokens(rows, name):
+            words = rows[:].bitcast(F32)
+            tiles = []
+            for g in range(PASSES):
+                bank = flip_psum.tile([P, BANK], F32, tag="flip")
+                for u in range(PAIR):
+                    for t in range(TOKENS // P):
+                        first_word = ROW_WORDS * t + P * PAIR * g
+                        nc.tensor.transpose(
+                            bank[:, TOKENS * u + P * t : TOKENS * u + P * (t + 1)],
+                            words[:, first_word + u : first_word + PAIR * P : PAIR],
+                            ident[:],
+                        )
+                by_k = keep.tile([P, TOKENS * PACK], BF16, name="%s%d" % (name, g), align_bytes=64)
+                empty_bank(
+                    g % 2 == 0,
+                    by_k[:].bitcast(F32).rearrange("p (t u) -> p t u", u=PAIR),
+                    bank[:].rearrange("p (u t) -> p t u", u=PAIR),
+                )
+                tiles.append(by_k)
+            return tiles
+
+        def group_view(tiles, j):
+            g, u = j // PAIR, j % PAIR
+            return tiles[g][:].rearrange("p (t c) -> p c t", c=PACK)[:, PAIR * u : PAIR * (u + 1), :]
+
+        x_codes = keep.tile([P, PASSES * TOKENS], U32, align_bytes=64)
+        x_scales = keep.tile([P, PASSES * TOKENS], U8, align_bytes=64)
+
+        def quantise_x():
+            for g in range(PASSES):
+                cols = slice(TOKENS * g, TOKENS * (g + 1))
+                nc.vector.quantize_mx(
+                    out=x_codes[:, cols].bitcast(FP8X4), scales=x_scales[:, cols], in_=x_by_k[g][:]
+                )
+
+        vector_count = len(vectors)
+        table = const.tile([P, PAIR * GROUPS * vector_count], F32)
+        z_b_half = const.tile([P, PAIR * GROUPS], F32)
+        a_work = const.tile([P, PAIR * GROUPS], F32)
+        a_neg = const.tile([P, PAIR * GROUPS], F32)
+        a_neg_dt_min = const.tile([P, PAIR * GROUPS], F32)
+
+        def transpose_vectors():
+            vector_bank = flip_psum.tile([P, BANK], F32, tag="flip")
+            words = vector_rows[:].bitcast(F32)
+            for u in range(PAIR):
+                nc.tensor.transpose(
+                    vector_bank[:, P * u : P * (u + 1)], words[:, u : PAIR * P : PAIR], ident[:]
+                )
+                rows = PASSES * vector_count
+                nc.vector.tensor_copy(
+                    out=table[:].rearrange("p (r u e) -> p r u e", u=PAIR, e=PAIR)[:, :, u, :],
+                    in_=vector_bank[:, P * u : P * u + rows]
+                    .bitcast(BF16)
+                    .rearrange("p (r e) -> p r e", e=PAIR),
+                )
+            nc.vector.tensor_scalar_mul(out=z_b_half[:], in0=rows_of(Z_B), scalar1=0.5)
+            nc.vector.tensor_scalar_min(out=a_work[:], in0=rows_of(A_BASE), scalar1=EXP_CAP)
+
+        def rows_of(which):
+            return table[:, PAIR * GROUPS * which : PAIR * GROUPS * (which + 1)]
+
+        def scalar_of(columns, j, e):
+            return columns[:, PAIR * j + e : PAIR * j + e + 1]
+
+        def group_tiles(name):
+            return [keep.tile([P, GROUP_COLS], F32, name="%s%d" % (name, j)) for j in range(GROUPS)]
+
+        def halves(group_tile):
+            return group_tile[:].rearrange("p (e t) -> p e t", e=PAIR)
+
+        soft = group_tiles("soft")
+        decay = group_tiles("decay")
+        state = group_tiles("state")
+        mix = group_tiles("mix")
+
+        banks = {}
+        grouped = {}
+        codes = {}
+        scales = {}
+        sums = {}
+
+        def transpose_row(index, e):
+            words = raw[index][:].bitcast(F32)
+            for b in range(BANKS_PER_ROW * e, BANKS_PER_ROW * (e + 1)):
+                bank = flip_psum.tile([P, BANK], F32, tag="flip")
+                for piece in range(BANK // P):
+                    first_word = BANK * b + P * PAIR * (piece // PAIR)
+                    u = piece % PAIR
+                    nc.tensor.transpose(
+                        bank[:, P * piece : P * (piece + 1)],
+                        words[:, first_word + u : first_word + PAIR * P : PAIR],
+                        ident[:],
+                    )
+                banks[index, b] = bank
+
+        def empty_group_bank(index, b):
+            empty_bank(
+                b == 0 and index < VECTOR_HELP_GROUPS,
+                grouped[index][:]
+                .bitcast(F32)[:, BANK * b : BANK * (b + 1)]
+                .rearrange("p (g n u) -> p g n u", g=PAIR, u=PAIR),
+                banks[index, b][:].rearrange("p (g u n) -> p g n u", g=PAIR, u=PAIR),
+            )
+
+        def quantise_group(index):
+            if GATES[index // GROUPS] == "c":
+                pool, suffix = keep, "_c%d" % (index % GROUPS)
+            else:
+                pool, suffix = mx_pool, ""
+            codes[index] = pool.tile(
+                [P, PAIR * PASSES * P], U32, name="codes" + suffix, align_bytes=64
+            )
+            scales[index] = pool.tile(
+                [P, PAIR * PASSES * P], U8, name="scales" + suffix, align_bytes=64
+            )
+            nc.vector.quantize_mx(
+                out=codes[index][:].bitcast(FP8X4), scales=scales[index][:], in_=grouped[index][:]
+            )
+
+        def multiply_row(index, e):
+            for g in range(PASSES):
+                w_cols = slice(P * (PASSES * e + g), P * (PASSES * e + g + 1))
+                x_cols = slice(TOKENS * g, TOKENS * (g + 1))
+                nc.tensor.matmul_mx(
+                    out=sums[index][:, TOKENS * e : TOKENS * (e + 1)],
+                    lhsT=codes[index][:, w_cols].bitcast(FP8X4),
+                    lhsT_scale=scales[index][:, w_cols],
+                    rhs=x_codes[:, x_cols].bitcast(FP8X4),
+                    rhs_scale=x_scales[:, x_cols],
+                    start=(g == 0),
+                    stop=(g == PASSES - 1),
+                )
+
+        def activate_sums(gate, j, out_tile, func, bias_columns, scale):
+            for e in range(PAIR):
+                cols = slice(TOKENS * e, TOKENS * (e + 1))
+                nc.scalar.activation(
+                    out=out_tile[:, cols],
+                    in_=sums[GROUPS * GATES.index(gate) + j][:, cols],
+                    func=func,
+                    bias=scalar_of(bias_columns, j, e),
+                    scale=scale,
+                )
+
+        def dt_argument(j):
+            activate_sums("dt", j, soft[j], ACT.Identity, rows_of(DT_B), 1.0)
+
+        def dt_cap(j):
+            nc.vector.tensor_scalar_min(out=decay[j][:], in0=soft[j][:], scalar1=EXP_CAP)
+
+        def dt_exp(j):
+            nc.scalar.activation(out=decay[j][:], in_=decay[j][:], func=ACT.Exp)
+
+        def dt_log(j):
+            nc.scalar.activation(out=decay[j][:], in_=decay[j][:], func=ACT.Ln, bias=one_col[:])
+
+        def dt_softplus(j):
+            nc.vector.tensor_tensor(out=soft[j][:], in0=soft[j][:], in1=decay[j][:], op=ALU.max)
+
+        def skip_minus_deter(j):
+            for e in range(PAIR):
+                nc.vector.scalar_tensor_tensor(
+                    out=halves(mix[j])[:, e, :],
+                    in0=group_view(x_by_k, j)[:, e, :],
+                    scalar=scalar_of(rows_of(SKIP), j, e),
+                    in1=group_view(deter_by_k, j)[:, e, :],
+                    op0=ALU.mult,
+                    op1=ALU.subtract,
+                )
+
+        def dt_times_x(j):
+            nc.vector.scalar_tensor_tensor(
+                out=halves(state[j]),
+                in0=halves(soft[j]),
+                scalar=DT_MIN,
+                in1=group_view(x_by_k, j),
+                op0=ALU.add,
+                op1=ALU.mult,
+            )
+
+        def decay_exp(j):
+            for e in range(PAIR):
+                cols = slice(TOKENS * e, TOKENS * (e + 1))
+                nc.scalar.activation(
+                    out=decay[j][:, cols],
+                    in_=soft[j][:, cols],
+                    func=ACT.Exp,
+                    bias=scalar_of(a_neg_dt_min, j, e),
+                    scale=scalar_of(a_neg, j, e),
+                )
+
+        def decay_times_deter(j):
+            nc.vector.tensor_tensor(
+                out=halves(decay[j]),
+                in0=halves(decay[j]),
+                in1=group_view(deter_by_k, j),
+                op=ALU.mult,
+            )
+
+        def c_matmuls(j):
+            index = GROUPS * GATES.index("c") + j
+            sums[index] = late_psum.tile([P, GROUP_COLS], F32, name="c_sums", tag="late")
+            for e in range(PAIR):
+                multiply_row(index, e)
+
+        b_gate = {}
+
+        def b_tanh(j):
+            b_gate[j] = temp.tile([P, GROUP_COLS], F32, name="b", tag="b")
+            activate_sums("b", j, b_gate[j], ACT.Tanh, rows_of(B_B), 1.0)
+
+        def input_term(j):
+            nc.vector.tensor_tensor(out=state[j][:], in0=state[j][:], in1=b_gate[j][:], op=ALU.mult)
+
+        def new_state(j):
+            nc.vector.tensor_tensor(out=state[j][:], in0=state[j][:], in1=decay[j][:], op=ALU.add)
+
+        def c_times_state(j):
+            for e in range(PAIR):
+                cols = slice(TOKENS * e, TOKENS * (e + 1))
+                nc.vector.scalar_tensor_tensor(
+                    out=state[j][:, cols],
+                    in0=sums[GROUPS * GATES.index("c") + j][:, cols],
+                    scalar=scalar_of(rows_of(C_B), j, e),
+                    in1=state[j][:, cols],
+                    op0=ALU.add,
+                    op1=ALU.mult,
+                )
+
+        def y_minus_deter(j):
+            nc.vector.tensor_tensor(out=mix[j][:], in0=mix[j][:], in1=state[j][:], op=ALU.add)
+
+        z_gate = {}
+
+        def z_tanh(j):
+            z_gate[j] = temp.tile([P, GROUP_COLS], F32, name="z", tag="z")
+            activate_sums("z", j, z_gate[j], ACT.Tanh, z_b_half, 0.5)
+
+        def gate_the_change(j):
+            nc.vector.scalar_tensor_tensor(
+                out=z_gate[j][:],
+                in0=z_gate[j][:],
+                scalar=1.0,
+                in1=mix[j][:],
+                op0=ALU.add,
+                op1=ALU.mult,
+            )
+
+        def add_deter(j):
+            nc.vector.scalar_tensor_tensor(
+                out=halves(mix[j]),
+                in0=halves(z_gate[j]),
+                scalar=0.5,
+                in1=group_view(deter_by_k, j),
+                op0=ALU.mult,
+                op1=ALU.add,
+            )
+
+        squares = {}
+
+        def square(j):
+            squares[j] = temp.tile([P, GROUP_COLS], F32, name="squares", tag="squares")
+            nc.scalar.activation(out=squares[j][:], in_=mix[j][:], func=ACT.Square)
+
+        token_tiles = TOKENS // P
+        totals = {}
+
+        def add_squares(j):
+            if j == 0:
+                totals[0] = late_psum.tile([P, BANK], F32, name="totals", tag="late")
+            for t in range(token_tiles):
+                first_col = ONES_COLS * (token_tiles * j + t)
+                for e in range(PAIR):
+                    first = TOKENS * e + P * t
+                    nc.tensor.matmul(
+                        out=totals[0][:, first_col : first_col + ONES_COLS],
+                        lhsT=squares[j][:, first : first + P],
+                        rhs=ones[:],
+                        start=(e == 0),
+                        stop=(e == PAIR - 1),
+                    )
+
+        def norm_gain(j):
+            for e in range(PAIR):
+                cols = slice(TOKENS * e, TOKENS * (e + 1))
+                nc.vector.tensor_scalar_mul(
+                    out=mix[j][:, cols], in0=mix[j][:, cols], scalar1=scalar_of(rows_of(NORM_W), j, e)
+                )
+
+        rms = const.tile([P, token_tiles], F32)
+        inv_rms = const.tile([P, token_tiles], F32)
+
+        def finish_norm():
+            square_sum = const.tile([P, token_tiles], F32)
+            nc.vector.tensor_reduce(
+                out=square_sum[:],
+                in_=totals[0][:].rearrange("p (j t c) -> p t j c", t=token_tiles, c=ONES_COLS)[
+                    :, :, :, 0
+                ],
+                axis=mybir.AxisListType.X,
+                op=ALU.add,
+            )
+            nc.scalar.activation(
+                out=rms[:], in_=square_sum[:], func=ACT.Sqrt, bias=eps_col[:], scale=1.0 / CHANNELS
+            )
+            nc.vector.reciprocal(out=inv_rms[:], in_=rms[:])
+
+        free_banks = (
+            FLIP_BANKS * [(flip_psum, "flip")]
+            + SUM_BANKS * [(sum_psum, "sums")]
+            + LATE_BANKS * [(late_psum, "late")]
+        )
+        groups_per_bank = BANK // GROUP_ROWS
+        out_banks = []
+
+        def flip_back(first_group):
+            for t in range(token_tiles):
+                pool, tag = free_banks[len(out_banks)]
+                bank = pool.tile([P, BANK], F32, name="out_bank", tag=tag)
+                for jj in range(groups_per_bank):
+                    for e in range(PAIR):
+                        first = TOKENS * e + P * t
+                        nc.tensor.transpose(
+                            bank[:, P * (PAIR * jj + e) : P * (PAIR * jj + e + 1)],
+                            mix[first_group + jj][:, first : first + P],
+                            ident[:],
+                        )
+                out_banks.append((bank, first_group, t))
+
+        def when_due(step, gate, lag, stage):
+            j = step - lag - GROUPS * GATES.index(gate)
+            if 0 <= j < GROUPS:
+                stage(j)
+
+        n_groups = len(GATES) * GROUPS
+        first_log_step = GROUPS + 5
+        logs_per_step = 2
+        last_group = n_groups - 1
+        deepest_lag = 11
+        for step in range(n_groups + deepest_lag):
+            if 1 <= step <= n_groups:
+                quantise_group(step - 1)
+
+            if step < n_groups:
+                for e in range(PAIR):
+                    transpose_row(step, e)
+            ready = step - MULTIPLY_LAG
+            if 0 <= ready < n_groups and GATES[ready // GROUPS] != "c":
+                sums[ready] = sum_psum.tile([P, GROUP_COLS], F32, name="sums", tag="sums")
+                for e in range(PAIR):
+                    multiply_row(ready, e)
+            if step < n_groups:
+                grouped[step] = grouped_pool.tile(
+                    [P, PAIR * CHANNELS], BF16, name="grouped", tag="grouped", align_bytes=64
+                )
+                for b in range(BANKS_PER_GROUP):
+                    empty_group_bank(step, b)
+            if step == 0:
+                x_by_k = transpose_tokens(x_rows, "x")
+            if step == 1:
+                quantise_x()
+            if step == 2:
+                deter_by_k = transpose_tokens(deter_rows, "deter")
+                transpose_vectors()
+            if step + LOADS_AHEAD < n_groups:
+                load_group(step + LOADS_AHEAD)
+
+            when_due(step, "dt", 3, dt_argument)
+            if step == 5:
+                nc.scalar.activation(out=a_work[:], in_=a_work[:], func=ACT.Exp)
+            when_due(step, "dt", 5, dt_exp)
+            log_step = step - first_log_step
+            if 0 <= log_step < GROUPS // logs_per_step:
+                if log_step == 0:
+                    nc.scalar.activation(out=a_work[:], in_=a_work[:], func=ACT.Ln, bias=one_col[:])
+                for j in range(logs_per_step * log_step, logs_per_step * (log_step + 1)):
+                    dt_log(j)
+            when_due(step, "b", 1, decay_exp)
+            when_due(step, "b", 3, b_tanh)
+            when_due(step, "z", 3, z_tanh)
+            when_due(step, "z", 6, square)
+            if step == last_group + 6:
+                nc.scalar.activation(out=sqrt_warm[:], in_=one_col[:], func=ACT.Sqrt)
+
+            when_due(step, "z", 11, norm_gain)
+            when_due(step, "z", 5, add_deter)
+            when_due(step, "z", 4, gate_the_change)
+            when_due(step, "b", 8, y_minus_deter)
+            when_due(step, "b", 6, c_times_state)
+            when_due(step, "b", 5, new_state)
+            when_due(step, "b", 4, input_term)
+            when_due(step, "b", 2, decay_times_deter)
+            when_due(step, "c", 7, dt_times_x)
+            if 1 <= log_step <= GROUPS // logs_per_step:
+                if log_step == 1:
+                    nc.vector.tensor_tensor(
+                        out=a_work[:], in0=a_work[:], in1=rows_of(A_BASE), op=ALU.max
+                    )
+                    nc.vector.tensor_scalar_mul(out=a_neg[:], in0=a_work[:], scalar1=-1.0)
+                    nc.vector.tensor_scalar_mul(out=a_neg_dt_min[:], in0=a_work[:], scalar1=-DT_MIN)
+                for j in range(logs_per_step * (log_step - 1), logs_per_step * log_step):
+                    dt_softplus(j)
+            when_due(step, "dt", 3, skip_minus_deter)
+            when_due(step, "dt", 4, dt_cap)
+
+            when_due(step, "b", 5, c_matmuls)
+            when_due(step, "z", 7, add_squares)
+
+        finish_norm()
+        for first_group in range(0, GROUPS, groups_per_bank):
+            flip_back(first_group)
+        for bank, first_group, t in out_banks:
+            normed = store_pool.tile([P, BANK], F32, tag="normed")
+            normed_view = normed[:].rearrange("p (c j e) -> p c j e", j=groups_per_bank, e=PAIR)
+            bank_view = bank[:].rearrange("p (j e c) -> p c j e", j=groups_per_bank, e=PAIR)
+            if t == 0:
+                nc.scalar.activation(
+                    out=normed_view, in_=bank_view, func=ACT.Copy, scale=inv_rms[:, t : t + 1]
+                )
+            else:
+                nc.vector.tensor_scalar_mul(
+                    out=normed_view, in0=bank_view, scalar1=inv_rms[:, t : t + 1]
+                )
+            first_channel = GROUP_ROWS * first_group
+            nc.sync.dma_start(
+                out=out[P * t : P * (t + 1), first_channel : first_channel + BANK], in_=normed[:]
+            )

@@ -24,15 +24,16 @@ ROW_WORDS = CHANNELS // PAIR
 BANK = 512
 BANKS_PER_ROW = ROW_WORDS // BANK
 BANKS_PER_GROUP = PAIR * BANKS_PER_ROW
+GROUP_WORDS = PAIR * PASSES * P
 
-GATES = ["dt", "c", "b", "z"]
-VECTOR_HELP_GROUPS = 20
+GATES = ["dt", "b", "c", "z"]
 MULTIPLY_LAG = 2
+SUMS_LAG = MULTIPLY_LAG + 1
 ONES_COLS = 32
 FLIP_BANKS = 5
 SUM_BANKS = 2
 LATE_BANKS = 1
-LOADS_AHEAD = 3
+LOADS_AHEAD = 4
 EPS = 1e-4
 DT_MIN = 1e-4
 EXP_CAP = 20.0
@@ -60,9 +61,9 @@ def tile_mamba2backbone_pb_kernel(
         keep = stack.enter_context(tc.tile_pool(name="keep", bufs=1))
         raw_pool = stack.enter_context(tc.tile_pool(name="raw", bufs=LOADS_AHEAD + 2))
         grouped_pool = stack.enter_context(tc.tile_pool(name="grouped", bufs=3))
-        mx_pool = stack.enter_context(tc.tile_pool(name="mx", bufs=2))
+        mx_pool = stack.enter_context(tc.tile_pool(name="mx", bufs=3))
         temp = stack.enter_context(tc.tile_pool(name="temp", bufs=3))
-        store_pool = stack.enter_context(tc.tile_pool(name="store", bufs=4))
+        store_pool = stack.enter_context(tc.tile_pool(name="store", bufs=8))
         flip_psum = stack.enter_context(tc.psum_pool(name="flip", bufs=FLIP_BANKS))
         sum_psum = stack.enter_context(tc.psum_pool(name="sums", bufs=SUM_BANKS))
         late_psum = stack.enter_context(tc.psum_pool(name="late", bufs=LATE_BANKS))
@@ -72,9 +73,10 @@ def tile_mamba2backbone_pb_kernel(
         make_identity(nc, ident[:])
         one_col = const.tile([P, 1], F32)
         nc.vector.memset(one_col[:], 1.0)
-        eps_col = const.tile([P, 1], F32)
-        nc.vector.memset(eps_col[:], EPS)
-        sqrt_warm = const.tile([P, 1], F32)
+        minus_half = const.tile([P, TOKENS // P], F32)
+        nc.vector.memset(minus_half[:], -0.5)
+        table_warm = const.tile([P, 1], F32)
+        nc.scalar.activation(out=table_warm[:], in_=one_col[:], func=ACT.Exp)
         ones = const.tile([P, ONES_COLS], F32)
         nc.vector.memset(ones[:], 1.0)
 
@@ -85,15 +87,24 @@ def tile_mamba2backbone_pb_kernel(
 
         raw = {}
 
-        def load_group(index):
+        def group_rows(index):
             gate, j = GATES[index // GROUPS], index % GROUPS
             g, u = j // PAIR, j % PAIR
             rows = weights[gate][P * PACK * g : P * PACK * (g + 1), :]
             rows = rows.rearrange("(p c) k -> p c k", c=PACK)
-            raw[index] = load_rows(rows[:, PAIR * u : PAIR * (u + 1), :])
+            return rows[:, PAIR * u : PAIR * (u + 1), :]
 
-        load_group(0)
+        def load_group(index):
+            rows = load_rows(group_rows(index))
+            raw[index] = [rows[:, CHANNELS * e : CHANNELS * (e + 1)] for e in range(PAIR)]
+
+        raw[0] = []
+        for e in range(PAIR):
+            first_rows = keep.tile([P, CHANNELS], BF16, name="first%d" % e)
+            nc.sync.dma_start(out=first_rows[:], in_=group_rows(0)[:, e, :])
+            raw[0].append(first_rows[:])
         x_rows = load_rows(x.rearrange("(t p) k -> p t k", p=P))
+        load_group(1)
         vector_rows = const.tile([P, PACK * P], BF16)
         nc.vector.memset(vector_rows[:], 0.0)
         for i, vector in enumerate(vectors):
@@ -101,9 +112,9 @@ def tile_mamba2backbone_pb_kernel(
                 out=vector_rows[PASSES * i : PASSES * (i + 1), :],
                 in_=vector.rearrange("(g c) -> g c", g=PASSES),
             )
-        load_group(1)
         load_group(2)
         deter_rows = load_rows(deter.rearrange("(t p) k -> p t k", p=P))
+        load_group(3)
 
         def empty_bank(on_vector, out_words, bank_view):
             if on_vector:
@@ -195,8 +206,8 @@ def tile_mamba2backbone_pb_kernel(
         sums = {}
 
         def transpose_row(index, e):
-            words = raw[index][:].bitcast(F32)
-            for b in range(BANKS_PER_ROW * e, BANKS_PER_ROW * (e + 1)):
+            words = raw[index][e].bitcast(F32)
+            for b in range(BANKS_PER_ROW):
                 bank = flip_psum.tile([P, BANK], F32, tag="flip")
                 for piece in range(BANK // P):
                     first_word = BANK * b + P * PAIR * (piece // PAIR)
@@ -206,31 +217,31 @@ def tile_mamba2backbone_pb_kernel(
                         words[:, first_word + u : first_word + PAIR * P : PAIR],
                         ident[:],
                     )
-                banks[index, b] = bank
+                banks[index, BANKS_PER_ROW * e + b] = bank
 
-        def empty_group_bank(index, b):
+        def empty_group_bank(index, b, on_vector):
             empty_bank(
-                b == 0 and index < VECTOR_HELP_GROUPS,
+                on_vector,
                 grouped[index][:]
                 .bitcast(F32)[:, BANK * b : BANK * (b + 1)]
                 .rearrange("p (g n u) -> p g n u", g=PAIR, u=PAIR),
                 banks[index, b][:].rearrange("p (g u n) -> p g n u", g=PAIR, u=PAIR),
             )
 
-        def quantise_group(index):
-            if GATES[index // GROUPS] == "c":
-                pool, suffix = keep, "_c%d" % (index % GROUPS)
-            else:
-                pool, suffix = mx_pool, ""
-            codes[index] = pool.tile(
-                [P, PAIR * PASSES * P], U32, name="codes" + suffix, align_bytes=64
-            )
-            scales[index] = pool.tile(
-                [P, PAIR * PASSES * P], U8, name="scales" + suffix, align_bytes=64
-            )
+        def quantise_columns(index, first, last):
             nc.vector.quantize_mx(
-                out=codes[index][:].bitcast(FP8X4), scales=scales[index][:], in_=grouped[index][:]
+                out=codes[index][:, first:last].bitcast(FP8X4),
+                scales=scales[index][:, first:last],
+                in_=grouped[index][:, PACK * first : PACK * last],
             )
+
+        def new_codes(index):
+            codes[index] = mx_pool.tile([P, GROUP_WORDS], U32, name="codes", align_bytes=64)
+            scales[index] = mx_pool.tile([P, GROUP_WORDS], U8, name="scales", align_bytes=64)
+
+        def quantise_group(index):
+            new_codes(index)
+            quantise_columns(index, 0, GROUP_WORDS)
 
         def multiply_row(index, e):
             for g in range(PASSES):
@@ -246,9 +257,14 @@ def tile_mamba2backbone_pb_kernel(
                     stop=(g == PASSES - 1),
                 )
 
-        def activate_sums(gate, j, out_tile, func, bias_columns, scale):
-            for e in range(PAIR):
-                cols = slice(TOKENS * e, TOKENS * (e + 1))
+        BOTH = (0, 1)
+
+        def columns_of(rows):
+            return slice(TOKENS * rows[0], TOKENS * (rows[-1] + 1))
+
+        def activate_sums(gate, j, out_tile, func, bias_columns, scale, rows=BOTH):
+            for e in rows:
+                cols = columns_of((e,))
                 nc.scalar.activation(
                     out=out_tile[:, cols],
                     in_=sums[GROUPS * GATES.index(gate) + j][:, cols],
@@ -312,16 +328,9 @@ def tile_mamba2backbone_pb_kernel(
                 op=ALU.mult,
             )
 
-        def c_matmuls(j):
-            index = GROUPS * GATES.index("c") + j
-            sums[index] = late_psum.tile([P, GROUP_COLS], F32, name="c_sums", tag="late")
-            for e in range(PAIR):
-                multiply_row(index, e)
-
-        b_gate = {}
+        b_gate = group_tiles("b")
 
         def b_tanh(j):
-            b_gate[j] = temp.tile([P, GROUP_COLS], F32, name="b", tag="b")
             activate_sums("b", j, b_gate[j], ACT.Tanh, rows_of(B_B), 1.0)
 
         def input_term(j):
@@ -347,35 +356,40 @@ def tile_mamba2backbone_pb_kernel(
 
         z_gate = {}
 
-        def z_tanh(j):
-            z_gate[j] = temp.tile([P, GROUP_COLS], F32, name="z", tag="z")
-            activate_sums("z", j, z_gate[j], ACT.Tanh, z_b_half, 0.5)
+        def z_tanh(j, rows=BOTH):
+            if j not in z_gate:
+                z_gate[j] = temp.tile([P, GROUP_COLS], F32, name="z", tag="z")
+            activate_sums("z", j, z_gate[j], ACT.Tanh, z_b_half, 0.5, rows)
 
-        def gate_the_change(j):
+        def gate_the_change(j, rows=BOTH):
+            cols = columns_of(rows)
             nc.vector.scalar_tensor_tensor(
-                out=z_gate[j][:],
-                in0=z_gate[j][:],
+                out=z_gate[j][:, cols],
+                in0=z_gate[j][:, cols],
                 scalar=1.0,
-                in1=mix[j][:],
+                in1=mix[j][:, cols],
                 op0=ALU.add,
                 op1=ALU.mult,
             )
 
-        def add_deter(j):
+        def add_deter(j, rows=BOTH):
+            some = slice(rows[0], rows[-1] + 1)
             nc.vector.scalar_tensor_tensor(
-                out=halves(mix[j]),
-                in0=halves(z_gate[j]),
+                out=halves(mix[j])[:, some, :],
+                in0=halves(z_gate[j])[:, some, :],
                 scalar=0.5,
-                in1=group_view(deter_by_k, j),
+                in1=group_view(deter_by_k, j)[:, some, :],
                 op0=ALU.mult,
                 op1=ALU.add,
             )
 
         squares = {}
 
-        def square(j):
-            squares[j] = temp.tile([P, GROUP_COLS], F32, name="squares", tag="squares")
-            nc.scalar.activation(out=squares[j][:], in_=mix[j][:], func=ACT.Square)
+        def square(j, rows=BOTH):
+            if j not in squares:
+                squares[j] = temp.tile([P, GROUP_COLS], F32, name="squares", tag="squares")
+            cols = columns_of(rows)
+            nc.scalar.activation(out=squares[j][:, cols], in_=mix[j][:, cols], func=ACT.Square)
 
         token_tiles = TOKENS // P
         totals = {}
@@ -402,7 +416,7 @@ def tile_mamba2backbone_pb_kernel(
                     out=mix[j][:, cols], in0=mix[j][:, cols], scalar1=scalar_of(rows_of(NORM_W), j, e)
                 )
 
-        rms = const.tile([P, token_tiles], F32)
+        mean_square = const.tile([P, token_tiles], F32)
         inv_rms = const.tile([P, token_tiles], F32)
 
         def finish_norm():
@@ -415,10 +429,17 @@ def tile_mamba2backbone_pb_kernel(
                 axis=mybir.AxisListType.X,
                 op=ALU.add,
             )
-            nc.scalar.activation(
-                out=rms[:], in_=square_sum[:], func=ACT.Sqrt, bias=eps_col[:], scale=1.0 / CHANNELS
+            nc.vector.tensor_scalar(
+                out=mean_square[:],
+                in0=square_sum[:],
+                scalar1=1.0 / CHANNELS,
+                scalar2=EPS,
+                op0=ALU.mult,
+                op1=ALU.add,
             )
-            nc.vector.reciprocal(out=inv_rms[:], in_=rms[:])
+            nc.gpsimd.tensor_tensor(
+                out=inv_rms[:], in0=mean_square[:], in1=minus_half[:], op=ALU.pow
+            )
 
         free_banks = (
             FLIP_BANKS * [(flip_psum, "flip")]
@@ -447,83 +468,154 @@ def tile_mamba2backbone_pb_kernel(
             if 0 <= j < GROUPS:
                 stage(j)
 
+        def multiply_group(index):
+            pool, tag = (late_psum, "late") if index == GROUPS + 2 else (sum_psum, "sums")
+            sums[index] = pool.tile([P, GROUP_COLS], F32, name="sums", tag=tag)
+            for e in range(PAIR):
+                multiply_row(index, e)
+
+        chain = []
+        for k in range(GROUPS + 3):
+            for stage, j in [
+                (dt_softplus, k),
+                (new_state, k - 3),
+                (input_term, k - 2),
+                (decay_times_deter, k - 2),
+                (dt_times_x, k - 1),
+            ]:
+                if 0 <= j < GROUPS:
+                    chain.append((stage, j))
+
         n_groups = len(GATES) * GROUPS
-        first_log_step = GROUPS + 5
-        logs_per_step = 2
         last_group = n_groups - 1
-        deepest_lag = 11
-        for step in range(n_groups + deepest_lag):
-            if 1 <= step <= n_groups:
+        log_step = GROUPS + SUMS_LAG
+        logs_in_step = {log_step: 3, log_step + 1: 5}
+        tanh_step = log_step + len(logs_in_step)
+        vector_banks = {log_step: 3, log_step + 1: 3, tanh_step: 2}
+        stage_slots = 4
+        logs_done = 0
+        decays_done = 0
+        softplus_done = 0
+        b_done = 0
+        multiplied = 0
+        for step in range(n_groups):
+            if step >= 1:
                 quantise_group(step - 1)
 
-            if step < n_groups:
-                for e in range(PAIR):
-                    transpose_row(step, e)
-            ready = step - MULTIPLY_LAG
-            if 0 <= ready < n_groups and GATES[ready // GROUPS] != "c":
-                sums[ready] = sum_psum.tile([P, GROUP_COLS], F32, name="sums", tag="sums")
-                for e in range(PAIR):
-                    multiply_row(ready, e)
-            if step < n_groups:
-                grouped[step] = grouped_pool.tile(
-                    [P, PAIR * CHANNELS], BF16, name="grouped", tag="grouped", align_bytes=64
-                )
-                for b in range(BANKS_PER_GROUP):
-                    empty_group_bank(step, b)
+            when_due(step, "dt", SUMS_LAG, dt_argument)
+            if step >= tanh_step:
+                while b_done < GROUPS and b_done + GROUPS + SUMS_LAG <= step:
+                    b_tanh(b_done)
+                    b_done += 1
+            when_due(step, "z", SUMS_LAG, z_tanh)
+            if step == last_group:
+                z_tanh(GROUPS - 3)
+
+            for e in range(PAIR):
+                transpose_row(step, e)
+            ready = step - (MULTIPLY_LAG if step < last_group - 1 else 1)
+            while multiplied <= ready:
+                multiply_group(multiplied)
+                multiplied += 1
+            when_due(step, "z", SUMS_LAG + 1, add_squares)
+            grouped[step] = grouped_pool.tile(
+                [P, PAIR * CHANNELS], BF16, name="grouped", tag="grouped", align_bytes=64
+            )
+
+            if step < GROUPS:
+                on_vector = 1
+            else:
+                on_vector = vector_banks.get(step, 0)
+            for b in range(BANKS_PER_GROUP):
+                empty_group_bank(step, b, b < on_vector)
+                if b == 1:
+                    if step >= tanh_step and decays_done < min(softplus_done, GROUPS):
+                        decay_exp(decays_done)
+                        decays_done += 1
+                    if step in logs_in_step:
+                        if logs_done == 0:
+                            nc.scalar.activation(
+                                out=a_work[:], in_=a_work[:], func=ACT.Ln, bias=one_col[:]
+                            )
+                        for j in range(logs_done, logs_done + logs_in_step[step]):
+                            dt_log(j)
+                        logs_done += logs_in_step[step]
+
             if step == 0:
                 x_by_k = transpose_tokens(x_rows, "x")
-            if step == 1:
                 quantise_x()
+            if step == 1:
+                transpose_vectors()
+                nc.scalar.activation(out=a_work[:], in_=a_work[:], func=ACT.Exp)
             if step == 2:
                 deter_by_k = transpose_tokens(deter_rows, "deter")
-                transpose_vectors()
             if step + LOADS_AHEAD < n_groups:
                 load_group(step + LOADS_AHEAD)
 
-            when_due(step, "dt", 3, dt_argument)
-            if step == 5:
-                nc.scalar.activation(out=a_work[:], in_=a_work[:], func=ACT.Exp)
-            when_due(step, "dt", 5, dt_exp)
-            log_step = step - first_log_step
-            if 0 <= log_step < GROUPS // logs_per_step:
-                if log_step == 0:
-                    nc.scalar.activation(out=a_work[:], in_=a_work[:], func=ACT.Ln, bias=one_col[:])
-                for j in range(logs_per_step * log_step, logs_per_step * (log_step + 1)):
-                    dt_log(j)
-            when_due(step, "b", 1, decay_exp)
-            when_due(step, "b", 3, b_tanh)
-            when_due(step, "z", 3, z_tanh)
-            when_due(step, "z", 6, square)
-            if step == last_group + 6:
-                nc.scalar.activation(out=sqrt_warm[:], in_=one_col[:], func=ACT.Sqrt)
+            used = on_vector
+            when_due(step, "c", SUMS_LAG, c_times_state)
+            if step >= 2 * GROUPS + SUMS_LAG:
+                used += 1
+            if step == log_step + 1:
+                nc.vector.tensor_tensor(
+                    out=a_work[:], in0=a_work[:], in1=rows_of(A_BASE), op=ALU.max
+                )
+                nc.vector.tensor_scalar_mul(out=a_neg[:], in0=a_work[:], scalar1=-1.0)
+                nc.vector.tensor_scalar_mul(out=a_neg_dt_min[:], in0=a_work[:], scalar1=-DT_MIN)
+            if step > log_step:
+                while chain and used < stage_slots:
+                    stage, j = chain[0]
+                    chain = chain[1:]
+                    stage(j)
+                    used += 1
+                    if stage == dt_softplus:
+                        softplus_done += 1
+            when_due(step, "dt", SUMS_LAG, dt_cap)
+            when_due(step, "dt", SUMS_LAG + 1, skip_minus_deter)
+            when_due(step, "z", SUMS_LAG, gate_the_change)
+            when_due(step, "z", -1, y_minus_deter)
+            if step == last_group:
+                gate_the_change(GROUPS - 3)
+            when_due(step, "z", SUMS_LAG, add_deter)
+            when_due(step, "z", SUMS_LAG + 1, norm_gain)
+            if step == last_group:
+                add_deter(GROUPS - 3)
 
-            when_due(step, "z", 11, norm_gain)
-            when_due(step, "z", 5, add_deter)
-            when_due(step, "z", 4, gate_the_change)
-            when_due(step, "b", 8, y_minus_deter)
-            when_due(step, "b", 6, c_times_state)
-            when_due(step, "b", 5, new_state)
-            when_due(step, "b", 4, input_term)
-            when_due(step, "b", 2, decay_times_deter)
-            when_due(step, "c", 7, dt_times_x)
-            if 1 <= log_step <= GROUPS // logs_per_step:
-                if log_step == 1:
-                    nc.vector.tensor_tensor(
-                        out=a_work[:], in0=a_work[:], in1=rows_of(A_BASE), op=ALU.max
-                    )
-                    nc.vector.tensor_scalar_mul(out=a_neg[:], in0=a_work[:], scalar1=-1.0)
-                    nc.vector.tensor_scalar_mul(out=a_neg_dt_min[:], in0=a_work[:], scalar1=-DT_MIN)
-                for j in range(logs_per_step * (log_step - 1), logs_per_step * log_step):
-                    dt_softplus(j)
-            when_due(step, "dt", 3, skip_minus_deter)
-            when_due(step, "dt", 4, dt_cap)
+            when_due(step, "dt", SUMS_LAG, dt_exp)
+            when_due(step, "z", SUMS_LAG, square)
+            if step == last_group:
+                square(GROUPS - 3)
 
-            when_due(step, "b", 5, c_matmuls)
-            when_due(step, "z", 7, add_squares)
+        j = GROUPS - 1
+        new_codes(last_group)
+        sums[last_group] = sum_psum.tile([P, GROUP_COLS], F32, name="sums", tag="sums")
+        for e in range(PAIR):
+            quantise_columns(last_group, GROUP_WORDS // PAIR * e, GROUP_WORDS // PAIR * (e + 1))
+            multiply_row(last_group, e)
+        flip_back(0)
+        flip_back(groups_per_bank)
+        for jj in (j - 3, j - 2):
+            add_squares(jj)
+            norm_gain(jj)
+        z_tanh(j - 1)
+        gate_the_change(j - 1)
+        z_tanh(j, (0,))
+        add_deter(j - 1)
+        z_tanh(j, (1,))
+        square(j - 1)
+        for e in range(PAIR):
+            gate_the_change(j, (e,))
+        for e in range(PAIR):
+            add_deter(j, (e,))
+            square(j, (e,))
 
+        add_squares(j - 1)
+        norm_gain(j - 1)
+        flip_back(GROUPS - 2 * groups_per_bank)
+        add_squares(j)
+        norm_gain(j)
         finish_norm()
-        for first_group in range(0, GROUPS, groups_per_bank):
-            flip_back(first_group)
+        flip_back(GROUPS - groups_per_bank)
         for bank, first_group, t in out_banks:
             normed = store_pool.tile([P, BANK], F32, tag="normed")
             normed_view = normed[:].rearrange("p (c j e) -> p c j e", j=groups_per_bank, e=PAIR)

@@ -29,14 +29,12 @@ GROUP_WORDS = PAIR * PASSES * P
 GATES = ["dt", "b", "c", "z"]
 MULTIPLY_LAG = 2
 SUMS_LAG = MULTIPLY_LAG + 1
-ONES_COLS = 32
 FLIP_BANKS = 5
-SUM_BANKS = 2
-LATE_BANKS = 1
+SUM_BANKS = 3
 LOADS_AHEAD = 4
 EPS = 1e-4
 DT_MIN = 1e-4
-EXP_CAP = 20.0
+FLOOR = 20.0
 
 A_BASE = 0
 DT_B = 1
@@ -44,7 +42,6 @@ B_B = 2
 C_B = 3
 Z_B = 4
 SKIP = 5
-NORM_W = 6
 
 FLOPS = 4 * 2 * TOKENS * CHANNELS * CHANNELS
 
@@ -54,7 +51,7 @@ def tile_mamba2backbone_pb_kernel(
 ):
     nc = tc.nc
     weights = {"dt": dt_w, "c": c_w, "b": b_w, "z": z_w}
-    vectors = [a_base, dt_b, b_b, c_b, z_b, skip, norm_w]
+    vectors = [a_base, dt_b, b_b, c_b, z_b, skip]
 
     with ExitStack() as stack:
         const = stack.enter_context(tc.tile_pool(name="const", bufs=1))
@@ -66,19 +63,18 @@ def tile_mamba2backbone_pb_kernel(
         store_pool = stack.enter_context(tc.tile_pool(name="store", bufs=8))
         flip_psum = stack.enter_context(tc.psum_pool(name="flip", bufs=FLIP_BANKS))
         sum_psum = stack.enter_context(tc.psum_pool(name="sums", bufs=SUM_BANKS))
-        late_psum = stack.enter_context(tc.psum_pool(name="late", bufs=LATE_BANKS))
         stack.enter_context(tc.manual_schedule())
 
         ident = const.tile([P, P], F32)
         make_identity(nc, ident[:])
         one_col = const.tile([P, 1], F32)
         nc.vector.memset(one_col[:], 1.0)
-        minus_half = const.tile([P, TOKENS // P], F32)
+        floor_col = const.tile([P, 1], F32)
+        nc.vector.memset(floor_col[:], -FLOOR)
+        minus_half = const.tile([P, 1], F32)
         nc.vector.memset(minus_half[:], -0.5)
         table_warm = const.tile([P, 1], F32)
-        nc.scalar.activation(out=table_warm[:], in_=one_col[:], func=ACT.Exp)
-        ones = const.tile([P, ONES_COLS], F32)
-        nc.vector.memset(ones[:], 1.0)
+        nc.scalar.activation(out=table_warm[:], in_=one_col[:], func=ACT.Sigmoid)
 
         def load_rows(rows_view):
             rows = raw_pool.tile([P, PAIR * CHANNELS], BF16, tag="raw")
@@ -86,6 +82,7 @@ def tile_mamba2backbone_pb_kernel(
             return rows
 
         raw = {}
+        norm_gain = const.tile([P, CHANNELS], BF16)
 
         def group_rows(index):
             gate, j = GATES[index // GROUPS], index % GROUPS
@@ -113,8 +110,8 @@ def tile_mamba2backbone_pb_kernel(
                 in_=vector.rearrange("(g c) -> g c", g=PASSES),
             )
         load_group(2)
-        deter_rows = load_rows(deter.rearrange("(t p) k -> p t k", p=P))
         load_group(3)
+        deter_rows = load_rows(deter.rearrange("(t p) k -> p t k", p=P))
 
         def empty_bank(on_vector, out_words, bank_view):
             if on_vector:
@@ -161,9 +158,11 @@ def tile_mamba2backbone_pb_kernel(
         vector_count = len(vectors)
         table = const.tile([P, PAIR * GROUPS * vector_count], F32)
         z_b_half = const.tile([P, PAIR * GROUPS], F32)
-        a_work = const.tile([P, PAIR * GROUPS], F32)
+        dt_b_raised = const.tile([P, PAIR * GROUPS], F32)
+        a_held = const.tile([P, PAIR * GROUPS], F32)
+        a_log = const.tile([P, PAIR * GROUPS], F32)
         a_neg = const.tile([P, PAIR * GROUPS], F32)
-        a_neg_dt_min = const.tile([P, PAIR * GROUPS], F32)
+        a_shift = const.tile([P, PAIR * GROUPS], F32)
 
         def transpose_vectors():
             vector_bank = flip_psum.tile([P, BANK], F32, tag="flip")
@@ -180,7 +179,8 @@ def tile_mamba2backbone_pb_kernel(
                     .rearrange("p (r e) -> p r e", e=PAIR),
                 )
             nc.vector.tensor_scalar_mul(out=z_b_half[:], in0=rows_of(Z_B), scalar1=0.5)
-            nc.vector.tensor_scalar_min(out=a_work[:], in0=rows_of(A_BASE), scalar1=EXP_CAP)
+            nc.vector.tensor_scalar_add(out=dt_b_raised[:], in0=rows_of(DT_B), scalar1=FLOOR)
+            nc.vector.tensor_scalar_max(out=a_held[:], in0=rows_of(A_BASE), scalar1=-FLOOR)
 
         def rows_of(which):
             return table[:, PAIR * GROUPS * which : PAIR * GROUPS * (which + 1)]
@@ -274,19 +274,20 @@ def tile_mamba2backbone_pb_kernel(
                 )
 
         def dt_argument(j):
-            activate_sums("dt", j, soft[j], ACT.Identity, rows_of(DT_B), 1.0)
+            activate_sums("dt", j, soft[j], ACT.Relu, dt_b_raised, 1.0)
 
-        def dt_cap(j):
-            nc.vector.tensor_scalar_min(out=decay[j][:], in0=soft[j][:], scalar1=EXP_CAP)
-
-        def dt_exp(j):
-            nc.scalar.activation(out=decay[j][:], in_=decay[j][:], func=ACT.Exp)
+        def dt_sigmoid(j):
+            nc.scalar.activation(
+                out=decay[j][:], in_=soft[j][:], func=ACT.Sigmoid, bias=floor_col[:]
+            )
 
         def dt_log(j):
-            nc.scalar.activation(out=decay[j][:], in_=decay[j][:], func=ACT.Ln, bias=one_col[:])
+            nc.scalar.activation(out=decay[j][:], in_=decay[j][:], func=ACT.Ln)
 
         def dt_softplus(j):
-            nc.vector.tensor_tensor(out=soft[j][:], in0=soft[j][:], in1=decay[j][:], op=ALU.max)
+            nc.vector.tensor_tensor(
+                out=soft[j][:], in0=soft[j][:], in1=decay[j][:], op=ALU.subtract
+            )
 
         def skip_minus_deter(j):
             for e in range(PAIR):
@@ -303,7 +304,7 @@ def tile_mamba2backbone_pb_kernel(
             nc.vector.scalar_tensor_tensor(
                 out=halves(state[j]),
                 in0=halves(soft[j]),
-                scalar=DT_MIN,
+                scalar=DT_MIN - FLOOR,
                 in1=group_view(x_by_k, j),
                 op0=ALU.add,
                 op1=ALU.mult,
@@ -316,7 +317,7 @@ def tile_mamba2backbone_pb_kernel(
                     out=decay[j][:, cols],
                     in_=soft[j][:, cols],
                     func=ACT.Exp,
-                    bias=scalar_of(a_neg_dt_min, j, e),
+                    bias=scalar_of(a_shift, j, e),
                     scale=scalar_of(a_neg, j, e),
                 )
 
@@ -383,85 +384,77 @@ def tile_mamba2backbone_pb_kernel(
                 op1=ALU.add,
             )
 
-        squares = {}
-
-        def square(j, rows=BOTH):
-            if j not in squares:
-                squares[j] = temp.tile([P, GROUP_COLS], F32, name="squares", tag="squares")
-            cols = columns_of(rows)
-            nc.scalar.activation(out=squares[j][:, cols], in_=mix[j][:, cols], func=ACT.Square)
-
         token_tiles = TOKENS // P
-        totals = {}
-
-        def add_squares(j):
-            if j == 0:
-                totals[0] = late_psum.tile([P, BANK], F32, name="totals", tag="late")
-            for t in range(token_tiles):
-                first_col = ONES_COLS * (token_tiles * j + t)
-                for e in range(PAIR):
-                    first = TOKENS * e + P * t
-                    nc.tensor.matmul(
-                        out=totals[0][:, first_col : first_col + ONES_COLS],
-                        lhsT=squares[j][:, first : first + P],
-                        rhs=ones[:],
-                        start=(e == 0),
-                        stop=(e == PAIR - 1),
-                    )
-
-        def norm_gain(j):
-            for e in range(PAIR):
-                cols = slice(TOKENS * e, TOKENS * (e + 1))
-                nc.vector.tensor_scalar_mul(
-                    out=mix[j][:, cols], in0=mix[j][:, cols], scalar1=scalar_of(rows_of(NORM_W), j, e)
-                )
-
+        groups_per_bank = BANK // GROUP_ROWS
+        pairs = GROUPS // groups_per_bank
+        square_sums = const.tile([P, token_tiles * pairs], F32)
         mean_square = const.tile([P, token_tiles], F32)
         inv_rms = const.tile([P, token_tiles], F32)
 
-        def finish_norm():
-            square_sum = const.tile([P, token_tiles], F32)
+        free_banks = FLIP_BANKS * [(flip_psum, "flip")] + SUM_BANKS * [(sum_psum, "sums")]
+        out_banks = {}
+
+        def flip_back(pair, t):
+            pool, tag = free_banks[len(out_banks)]
+            bank = pool.tile([P, BANK], F32, name="out_bank", tag=tag)
+            for jj in range(groups_per_bank):
+                for e in range(PAIR):
+                    first = TOKENS * e + P * t
+                    nc.tensor.transpose(
+                        bank[:, P * (PAIR * jj + e) : P * (PAIR * jj + e + 1)],
+                        mix[groups_per_bank * pair + jj][:, first : first + P],
+                        ident[:],
+                    )
+            out_banks[pair, t] = bank
+
+        def add_squares(pair, t):
+            squares = temp.tile([P, BANK], F32, name="squares", tag="squares")
+            column = pairs * t + pair
+            nc.scalar.activation(
+                out=squares[:],
+                in_=out_banks[pair, t][:],
+                func=ACT.Square,
+                accum_out=square_sums[:, column : column + 1],
+            )
+
+        def finish_norm(t):
+            total = const.tile([P, 1], F32, name="total%d" % t)
             nc.vector.tensor_reduce(
-                out=square_sum[:],
-                in_=totals[0][:].rearrange("p (j t c) -> p t j c", t=token_tiles, c=ONES_COLS)[
-                    :, :, :, 0
-                ],
+                out=total[:],
+                in_=square_sums[:, pairs * t : pairs * (t + 1)],
                 axis=mybir.AxisListType.X,
                 op=ALU.add,
             )
             nc.vector.tensor_scalar(
-                out=mean_square[:],
-                in0=square_sum[:],
+                out=mean_square[:, t : t + 1],
+                in0=total[:],
                 scalar1=1.0 / CHANNELS,
                 scalar2=EPS,
                 op0=ALU.mult,
                 op1=ALU.add,
             )
             nc.gpsimd.tensor_tensor(
-                out=inv_rms[:], in0=mean_square[:], in1=minus_half[:], op=ALU.pow
+                out=inv_rms[:, t : t + 1],
+                in0=mean_square[:, t : t + 1],
+                in1=minus_half[:],
+                op=ALU.pow,
             )
 
-        free_banks = (
-            FLIP_BANKS * [(flip_psum, "flip")]
-            + SUM_BANKS * [(sum_psum, "sums")]
-            + LATE_BANKS * [(late_psum, "late")]
-        )
-        groups_per_bank = BANK // GROUP_ROWS
-        out_banks = []
-
-        def flip_back(first_group):
-            for t in range(token_tiles):
-                pool, tag = free_banks[len(out_banks)]
-                bank = pool.tile([P, BANK], F32, name="out_bank", tag=tag)
-                for jj in range(groups_per_bank):
-                    for e in range(PAIR):
-                        first = TOKENS * e + P * t
-                        nc.tensor.transpose(
-                            bank[:, P * (PAIR * jj + e) : P * (PAIR * jj + e + 1)],
-                            mix[first_group + jj][:, first : first + P],
-                            ident[:],
-                        )
-                out_banks.append((bank, first_group, t))
+        def store(pair, t):
+            channels = slice(BANK * pair, BANK * (pair + 1))
+            normed = store_pool.tile([P, BANK], F32, tag="normed")
+            by_channel = "p (c j e) -> p c j e"
+            nc.vector.scalar_tensor_tensor(
+                out=normed[:].rearrange(by_channel, j=groups_per_bank, e=PAIR),
+                in0=out_banks[pair, t][:].rearrange(
+                    "p (j e c) -> p c j e", j=groups_per_bank, e=PAIR
+                ),
+                scalar=inv_rms[:, t : t + 1],
+                in1=norm_gain[:, channels].rearrange(by_channel, j=groups_per_bank, e=PAIR),
+                op0=ALU.mult,
+                op1=ALU.mult,
+            )
+            nc.sync.dma_start(out=out[P * t : P * (t + 1), channels], in_=normed[:])
 
         def when_due(step, gate, lag, stage):
             j = step - lag - GROUPS * GATES.index(gate)
@@ -469,8 +462,7 @@ def tile_mamba2backbone_pb_kernel(
                 stage(j)
 
         def multiply_group(index):
-            pool, tag = (late_psum, "late") if index == GROUPS + 2 else (sum_psum, "sums")
-            sums[index] = pool.tile([P, GROUP_COLS], F32, name="sums", tag=tag)
+            sums[index] = sum_psum.tile([P, GROUP_COLS], F32, name="sums", tag="sums")
             for e in range(PAIR):
                 multiply_row(index, e)
 
@@ -492,7 +484,6 @@ def tile_mamba2backbone_pb_kernel(
         logs_in_step = {log_step: 3, log_step + 1: 5}
         tanh_step = log_step + len(logs_in_step)
         vector_banks = {log_step: 3, log_step + 1: 3, tanh_step: 2}
-        stage_slots = 4
         logs_done = 0
         decays_done = 0
         softplus_done = 0
@@ -513,11 +504,10 @@ def tile_mamba2backbone_pb_kernel(
 
             for e in range(PAIR):
                 transpose_row(step, e)
-            ready = step - (MULTIPLY_LAG if step < last_group - 1 else 1)
+            ready = step - (MULTIPLY_LAG if 4 <= step < last_group - 1 else 1)
             while multiplied <= ready:
                 multiply_group(multiplied)
                 multiplied += 1
-            when_due(step, "z", SUMS_LAG + 1, add_squares)
             grouped[step] = grouped_pool.tile(
                 [P, PAIR * CHANNELS], BF16, name="grouped", tag="grouped", align_bytes=64
             )
@@ -534,9 +524,7 @@ def tile_mamba2backbone_pb_kernel(
                         decays_done += 1
                     if step in logs_in_step:
                         if logs_done == 0:
-                            nc.scalar.activation(
-                                out=a_work[:], in_=a_work[:], func=ACT.Ln, bias=one_col[:]
-                            )
+                            nc.scalar.activation(out=a_log[:], in_=a_log[:], func=ACT.Ln)
                         for j in range(logs_done, logs_done + logs_in_step[step]):
                             dt_log(j)
                         logs_done += logs_in_step[step]
@@ -546,45 +534,39 @@ def tile_mamba2backbone_pb_kernel(
                 quantise_x()
             if step == 1:
                 transpose_vectors()
-                nc.scalar.activation(out=a_work[:], in_=a_work[:], func=ACT.Exp)
-            if step == 2:
+                nc.scalar.activation(out=a_log[:], in_=a_held[:], func=ACT.Sigmoid)
+            if step == 3:
                 deter_by_k = transpose_tokens(deter_rows, "deter")
             if step + LOADS_AHEAD < n_groups:
                 load_group(step + LOADS_AHEAD)
+            if step == GROUPS:
+                nc.sync.dma_start(out=norm_gain[:], in_=norm_w.partition_broadcast(P))
 
-            used = on_vector
             when_due(step, "c", SUMS_LAG, c_times_state)
-            if step >= 2 * GROUPS + SUMS_LAG:
-                used += 1
             if step == log_step + 1:
                 nc.vector.tensor_tensor(
-                    out=a_work[:], in0=a_work[:], in1=rows_of(A_BASE), op=ALU.max
+                    out=a_neg[:], in0=a_log[:], in1=a_held[:], op=ALU.subtract
                 )
-                nc.vector.tensor_scalar_mul(out=a_neg[:], in0=a_work[:], scalar1=-1.0)
-                nc.vector.tensor_scalar_mul(out=a_neg_dt_min[:], in0=a_work[:], scalar1=-DT_MIN)
+                nc.vector.tensor_scalar_mul(
+                    out=a_shift[:], in0=a_neg[:], scalar1=DT_MIN - FLOOR
+                )
             if step > log_step:
-                while chain and used < stage_slots:
-                    stage, j = chain[0]
-                    chain = chain[1:]
+                slots = (4 if step < 2 * GROUPS else 3) - on_vector
+                due, chain = chain[:slots], chain[slots:]
+                for stage, j in due:
                     stage(j)
-                    used += 1
                     if stage == dt_softplus:
                         softplus_done += 1
-            when_due(step, "dt", SUMS_LAG, dt_cap)
             when_due(step, "dt", SUMS_LAG + 1, skip_minus_deter)
             when_due(step, "z", SUMS_LAG, gate_the_change)
             when_due(step, "z", -1, y_minus_deter)
             if step == last_group:
                 gate_the_change(GROUPS - 3)
             when_due(step, "z", SUMS_LAG, add_deter)
-            when_due(step, "z", SUMS_LAG + 1, norm_gain)
             if step == last_group:
                 add_deter(GROUPS - 3)
 
-            when_due(step, "dt", SUMS_LAG, dt_exp)
-            when_due(step, "z", SUMS_LAG, square)
-            if step == last_group:
-                square(GROUPS - 3)
+            when_due(step, "dt", SUMS_LAG, dt_sigmoid)
 
         j = GROUPS - 1
         new_codes(last_group)
@@ -592,43 +574,23 @@ def tile_mamba2backbone_pb_kernel(
         for e in range(PAIR):
             quantise_columns(last_group, GROUP_WORDS // PAIR * e, GROUP_WORDS // PAIR * (e + 1))
             multiply_row(last_group, e)
-        flip_back(0)
-        flip_back(groups_per_bank)
-        for jj in (j - 3, j - 2):
-            add_squares(jj)
-            norm_gain(jj)
         z_tanh(j - 1)
         gate_the_change(j - 1)
-        z_tanh(j, (0,))
+        for e in range(PAIR):
+            z_tanh(j, (e,))
         add_deter(j - 1)
-        z_tanh(j, (1,))
-        square(j - 1)
         for e in range(PAIR):
             gate_the_change(j, (e,))
         for e in range(PAIR):
             add_deter(j, (e,))
-            square(j, (e,))
-
-        add_squares(j - 1)
-        norm_gain(j - 1)
-        flip_back(GROUPS - 2 * groups_per_bank)
-        add_squares(j)
-        norm_gain(j)
-        finish_norm()
-        flip_back(GROUPS - groups_per_bank)
-        for bank, first_group, t in out_banks:
-            normed = store_pool.tile([P, BANK], F32, tag="normed")
-            normed_view = normed[:].rearrange("p (c j e) -> p c j e", j=groups_per_bank, e=PAIR)
-            bank_view = bank[:].rearrange("p (j e c) -> p c j e", j=groups_per_bank, e=PAIR)
-            if t == 0:
-                nc.scalar.activation(
-                    out=normed_view, in_=bank_view, func=ACT.Copy, scale=inv_rms[:, t : t + 1]
-                )
-            else:
-                nc.vector.tensor_scalar_mul(
-                    out=normed_view, in0=bank_view, scalar1=inv_rms[:, t : t + 1]
-                )
-            first_channel = GROUP_ROWS * first_group
-            nc.sync.dma_start(
-                out=out[P * t : P * (t + 1), first_channel : first_channel + BANK], in_=normed[:]
-            )
+        for t in range(token_tiles):
+            for pair in range(pairs - 1):
+                flip_back(pair, t)
+        for t in range(token_tiles):
+            flip_back(pairs - 1, t)
+        for t in range(token_tiles):
+            for pair in range(pairs):
+                add_squares(pair, t)
+            finish_norm(t)
+            for pair in range(pairs):
+                store(pair, t)

@@ -60,7 +60,6 @@ def tile_mamba2backbone_pb_kernel(
         grouped_pool = stack.enter_context(tc.tile_pool(name="grouped", bufs=3))
         mx_pool = stack.enter_context(tc.tile_pool(name="mx", bufs=3))
         temp = stack.enter_context(tc.tile_pool(name="temp", bufs=3))
-        store_pool = stack.enter_context(tc.tile_pool(name="store", bufs=8))
         flip_psum = stack.enter_context(tc.psum_pool(name="flip", bufs=FLIP_BANKS))
         sum_psum = stack.enter_context(tc.psum_pool(name="sums", bufs=SUM_BANKS))
         stack.enter_context(tc.manual_schedule())
@@ -82,6 +81,7 @@ def tile_mamba2backbone_pb_kernel(
             return rows
 
         raw = {}
+
         norm_gain = const.tile([P, CHANNELS], BF16)
 
         def group_rows(index):
@@ -93,13 +93,17 @@ def tile_mamba2backbone_pb_kernel(
 
         def load_group(index):
             rows = load_rows(group_rows(index))
-            raw[index] = [rows[:, CHANNELS * e : CHANNELS * (e + 1)] for e in range(PAIR)]
+            raw[index] = [
+                rows[:, PAIR * BANK * b : PAIR * BANK * (b + 1)] for b in range(BANKS_PER_GROUP)
+            ]
 
+        bank_values = PAIR * BANK
         raw[0] = []
-        for e in range(PAIR):
-            first_rows = keep.tile([P, CHANNELS], BF16, name="first%d" % e)
-            nc.sync.dma_start(out=first_rows[:], in_=group_rows(0)[:, e, :])
-            raw[0].append(first_rows[:])
+        for e, first, last in [(0, 0, bank_values), (0, bank_values, CHANNELS), (1, 0, CHANNELS)]:
+            first_rows = keep.tile([P, last - first], BF16, name="first%d_%d" % (e, first))
+            nc.sync.dma_start(out=first_rows[:], in_=group_rows(0)[:, e, first:last])
+            for start in range(0, last - first, bank_values):
+                raw[0].append(first_rows[:, start : start + bank_values])
         x_rows = load_rows(x.rearrange("(t p) k -> p t k", p=P))
         load_group(1)
         vector_rows = const.tile([P, PACK * P], BF16)
@@ -205,19 +209,18 @@ def tile_mamba2backbone_pb_kernel(
         scales = {}
         sums = {}
 
-        def transpose_row(index, e):
-            words = raw[index][e].bitcast(F32)
-            for b in range(BANKS_PER_ROW):
-                bank = flip_psum.tile([P, BANK], F32, tag="flip")
-                for piece in range(BANK // P):
-                    first_word = BANK * b + P * PAIR * (piece // PAIR)
-                    u = piece % PAIR
-                    nc.tensor.transpose(
-                        bank[:, P * piece : P * (piece + 1)],
-                        words[:, first_word + u : first_word + PAIR * P : PAIR],
-                        ident[:],
-                    )
-                banks[index, BANKS_PER_ROW * e + b] = bank
+        def transpose_bank(index, b):
+            words = raw[index][b].bitcast(F32)
+            bank = flip_psum.tile([P, BANK], F32, tag="flip")
+            for piece in range(BANK // P):
+                first_word = P * PAIR * (piece // PAIR)
+                u = piece % PAIR
+                nc.tensor.transpose(
+                    bank[:, P * piece : P * (piece + 1)],
+                    words[:, first_word + u : first_word + PAIR * P : PAIR],
+                    ident[:],
+                )
+            banks[index, b] = bank
 
         def empty_group_bank(index, b, on_vector):
             empty_bank(
@@ -243,12 +246,14 @@ def tile_mamba2backbone_pb_kernel(
             new_codes(index)
             quantise_columns(index, 0, GROUP_WORDS)
 
-        def multiply_row(index, e):
+        ALL = slice(0, TOKENS)
+
+        def multiply_row(index, e, tokens=ALL):
             for g in range(PASSES):
                 w_cols = slice(P * (PASSES * e + g), P * (PASSES * e + g + 1))
-                x_cols = slice(TOKENS * g, TOKENS * (g + 1))
+                x_cols = slice(TOKENS * g + tokens.start, TOKENS * g + tokens.stop)
                 nc.tensor.matmul_mx(
-                    out=sums[index][:, TOKENS * e : TOKENS * (e + 1)],
+                    out=sums[index][:, TOKENS * e + tokens.start : TOKENS * e + tokens.stop],
                     lhsT=codes[index][:, w_cols].bitcast(FP8X4),
                     lhsT_scale=scales[index][:, w_cols],
                     rhs=x_codes[:, x_cols].bitcast(FP8X4),
@@ -257,14 +262,9 @@ def tile_mamba2backbone_pb_kernel(
                     stop=(g == PASSES - 1),
                 )
 
-        BOTH = (0, 1)
-
-        def columns_of(rows):
-            return slice(TOKENS * rows[0], TOKENS * (rows[-1] + 1))
-
-        def activate_sums(gate, j, out_tile, func, bias_columns, scale, rows=BOTH):
-            for e in rows:
-                cols = columns_of((e,))
+        def activate_sums(gate, j, out_tile, func, bias_columns, scale, tokens=ALL):
+            for e in range(PAIR):
+                cols = slice(TOKENS * e + tokens.start, TOKENS * e + tokens.stop)
                 nc.scalar.activation(
                     out=out_tile[:, cols],
                     in_=sums[GROUPS * GATES.index(gate) + j][:, cols],
@@ -357,29 +357,27 @@ def tile_mamba2backbone_pb_kernel(
 
         z_gate = {}
 
-        def z_tanh(j, rows=BOTH):
+        def z_tanh(j, tokens=ALL):
             if j not in z_gate:
                 z_gate[j] = temp.tile([P, GROUP_COLS], F32, name="z", tag="z")
-            activate_sums("z", j, z_gate[j], ACT.Tanh, z_b_half, 0.5, rows)
+            activate_sums("z", j, z_gate[j], ACT.Tanh, z_b_half, 0.5, tokens)
 
-        def gate_the_change(j, rows=BOTH):
-            cols = columns_of(rows)
+        def gate_the_change(j, tokens=ALL):
             nc.vector.scalar_tensor_tensor(
-                out=z_gate[j][:, cols],
-                in0=z_gate[j][:, cols],
+                out=halves(z_gate[j])[:, :, tokens],
+                in0=halves(z_gate[j])[:, :, tokens],
                 scalar=1.0,
-                in1=mix[j][:, cols],
+                in1=halves(mix[j])[:, :, tokens],
                 op0=ALU.add,
                 op1=ALU.mult,
             )
 
-        def add_deter(j, rows=BOTH):
-            some = slice(rows[0], rows[-1] + 1)
+        def add_deter(j, tokens=ALL):
             nc.vector.scalar_tensor_tensor(
-                out=halves(mix[j])[:, some, :],
-                in0=halves(z_gate[j])[:, some, :],
+                out=halves(mix[j])[:, :, tokens],
+                in0=halves(z_gate[j])[:, :, tokens],
                 scalar=0.5,
-                in1=group_view(deter_by_k, j)[:, some, :],
+                in1=group_view(deter_by_k, j)[:, :, tokens],
                 op0=ALU.mult,
                 op1=ALU.add,
             )
@@ -387,8 +385,9 @@ def tile_mamba2backbone_pb_kernel(
         token_tiles = TOKENS // P
         groups_per_bank = BANK // GROUP_ROWS
         pairs = GROUPS // groups_per_bank
-        square_sums = const.tile([P, token_tiles * pairs], F32)
-        mean_square = const.tile([P, token_tiles], F32)
+        parts = pairs + 1
+        mean_square_parts = const.tile([P, token_tiles * parts], F32)
+        nc.vector.memset(mean_square_parts[:], EPS)
         inv_rms = const.tile([P, token_tiles], F32)
 
         free_banks = FLIP_BANKS * [(flip_psum, "flip")] + SUM_BANKS * [(sum_psum, "sums")]
@@ -409,43 +408,37 @@ def tile_mamba2backbone_pb_kernel(
 
         def add_squares(pair, t):
             squares = temp.tile([P, BANK], F32, name="squares", tag="squares")
-            column = pairs * t + pair
+            column = parts * t + pair
             nc.scalar.activation(
                 out=squares[:],
                 in_=out_banks[pair, t][:],
                 func=ACT.Square,
-                accum_out=square_sums[:, column : column + 1],
+                scale=CHANNELS**-0.5,
+                accum_out=mean_square_parts[:, column : column + 1],
             )
 
         def finish_norm(t):
-            total = const.tile([P, 1], F32, name="total%d" % t)
+            mean_square = const.tile([P, 1], F32, name="mean_square%d" % t)
             nc.vector.tensor_reduce(
-                out=total[:],
-                in_=square_sums[:, pairs * t : pairs * (t + 1)],
+                out=mean_square[:],
+                in_=mean_square_parts[:, parts * t : parts * (t + 1)],
                 axis=mybir.AxisListType.X,
                 op=ALU.add,
             )
-            nc.vector.tensor_scalar(
-                out=mean_square[:, t : t + 1],
-                in0=total[:],
-                scalar1=1.0 / CHANNELS,
-                scalar2=EPS,
-                op0=ALU.mult,
-                op1=ALU.add,
-            )
             nc.gpsimd.tensor_tensor(
-                out=inv_rms[:, t : t + 1],
-                in0=mean_square[:, t : t + 1],
-                in1=minus_half[:],
-                op=ALU.pow,
+                out=inv_rms[:, t : t + 1], in0=mean_square[:], in1=minus_half[:], op=ALU.pow
             )
+
+        normed_rows = {}
 
         def store(pair, t):
             channels = slice(BANK * pair, BANK * (pair + 1))
-            normed = store_pool.tile([P, BANK], F32, tag="normed")
+            if pair == 0:
+                normed_rows[t] = raw_pool.tile([P, PAIR * CHANNELS], BF16, name="normed", tag="raw")
+            normed = normed_rows[t][:].bitcast(F32)[:, channels]
             by_channel = "p (c j e) -> p c j e"
             nc.vector.scalar_tensor_tensor(
-                out=normed[:].rearrange(by_channel, j=groups_per_bank, e=PAIR),
+                out=normed.rearrange(by_channel, j=groups_per_bank, e=PAIR),
                 in0=out_banks[pair, t][:].rearrange(
                     "p (j e c) -> p c j e", j=groups_per_bank, e=PAIR
                 ),
@@ -454,7 +447,7 @@ def tile_mamba2backbone_pb_kernel(
                 op0=ALU.mult,
                 op1=ALU.mult,
             )
-            nc.sync.dma_start(out=out[P * t : P * (t + 1), channels], in_=normed[:])
+            nc.sync.dma_start(out=out[P * t : P * (t + 1), channels], in_=normed)
 
         def when_due(step, gate, lag, stage):
             j = step - lag - GROUPS * GATES.index(gate)
@@ -490,7 +483,7 @@ def tile_mamba2backbone_pb_kernel(
         b_done = 0
         multiplied = 0
         for step in range(n_groups):
-            if step >= 1:
+            if step >= 2:
                 quantise_group(step - 1)
 
             when_due(step, "dt", SUMS_LAG, dt_argument)
@@ -502,8 +495,8 @@ def tile_mamba2backbone_pb_kernel(
             if step == last_group:
                 z_tanh(GROUPS - 3)
 
-            for e in range(PAIR):
-                transpose_row(step, e)
+            for b in range(BANKS_PER_GROUP):
+                transpose_bank(step, b)
             ready = step - (MULTIPLY_LAG if 4 <= step < last_group - 1 else 1)
             while multiplied <= ready:
                 multiply_group(multiplied)
@@ -530,6 +523,7 @@ def tile_mamba2backbone_pb_kernel(
                         logs_done += logs_in_step[step]
 
             if step == 0:
+                quantise_group(0)
                 x_by_k = transpose_tokens(x_rows, "x")
                 quantise_x()
             if step == 1:
@@ -563,34 +557,44 @@ def tile_mamba2backbone_pb_kernel(
             if step == last_group:
                 gate_the_change(GROUPS - 3)
             when_due(step, "z", SUMS_LAG, add_deter)
-            if step == last_group:
-                add_deter(GROUPS - 3)
 
             when_due(step, "dt", SUMS_LAG, dt_sigmoid)
 
         j = GROUPS - 1
+        last_pair = pairs - 1
+        tiles = [slice(P * t, P * (t + 1)) for t in range(token_tiles)]
         new_codes(last_group)
         sums[last_group] = sum_psum.tile([P, GROUP_COLS], F32, name="sums", tag="sums")
-        for e in range(PAIR):
-            quantise_columns(last_group, GROUP_WORDS // PAIR * e, GROUP_WORDS // PAIR * (e + 1))
-            multiply_row(last_group, e)
+        half_words = GROUP_WORDS // PAIR
+        quantise_columns(last_group, 0, half_words)
+        add_deter(j - 2)
+        quantise_columns(last_group, half_words, GROUP_WORDS)
+        flip_back(0, 0)
+        flip_back(1, 0)
+        for tokens in tiles:
+            for e in range(PAIR):
+                multiply_row(last_group, e, tokens)
         z_tanh(j - 1)
         gate_the_change(j - 1)
-        for e in range(PAIR):
-            z_tanh(j, (e,))
         add_deter(j - 1)
-        for e in range(PAIR):
-            gate_the_change(j, (e,))
-        for e in range(PAIR):
-            add_deter(j, (e,))
-        for t in range(token_tiles):
-            for pair in range(pairs - 1):
-                flip_back(pair, t)
-        for t in range(token_tiles):
-            flip_back(pairs - 1, t)
-        for t in range(token_tiles):
-            for pair in range(pairs):
-                add_squares(pair, t)
-            finish_norm(t)
-            for pair in range(pairs):
-                store(pair, t)
+        add_squares(0, 0)
+        z_tanh(j, tiles[0])
+        gate_the_change(j, tiles[0])
+        add_deter(j, tiles[0])
+        add_squares(1, 0)
+        z_tanh(j, tiles[1])
+        gate_the_change(j, tiles[1])
+        add_deter(j, tiles[1])
+        for pair, t in [(2, 0), (0, 1), (1, 1), (last_pair, 0), (2, 1), (last_pair, 1)]:
+            flip_back(pair, t)
+        for pair, t in [(2, 0), (0, 1), (last_pair, 0)]:
+            add_squares(pair, t)
+        finish_norm(0)
+        for pair in range(1, pairs):
+            add_squares(pair, 1)
+        for pair in range(pairs):
+            store(pair, 0)
+            if pair == 1:
+                finish_norm(1)
+        for pair in range(pairs):
+            store(pair, 1)

@@ -454,11 +454,6 @@ def tile_mamba2backbone_pb_kernel(
             if 0 <= j < GROUPS:
                 stage(j)
 
-        def multiply_group(index):
-            sums[index] = sum_psum.tile([P, GROUP_COLS], F32, name="sums", tag="sums")
-            for e in range(PAIR):
-                multiply_row(index, e)
-
         chain = []
         for k in range(GROUPS + 3):
             for stage, j in [
@@ -476,7 +471,7 @@ def tile_mamba2backbone_pb_kernel(
         log_step = GROUPS + SUMS_LAG
         logs_in_step = {log_step: 3, log_step + 1: 5}
         tanh_step = log_step + len(logs_in_step)
-        vector_banks = {log_step: 3, log_step + 1: 3, tanh_step: 2}
+        vector_banks = {log_step: 4, log_step + 1: 4, tanh_step: 2}
         logs_done = 0
         decays_done = 0
         softplus_done = 0
@@ -495,12 +490,22 @@ def tile_mamba2backbone_pb_kernel(
             if step == last_group:
                 z_tanh(GROUPS - 3)
 
-            for b in range(BANKS_PER_GROUP):
-                transpose_bank(step, b)
-            ready = step - (MULTIPLY_LAG if 4 <= step < last_group - 1 else 1)
-            while multiplied <= ready:
-                multiply_group(multiplied)
-                multiplied += 1
+            lag = MULTIPLY_LAG if 4 <= step < last_group - 1 else 1
+            due = range(multiplied, step - lag + 1)
+            multiplied = max(multiplied, step - lag + 1)
+            for index in due:
+                sums[index] = sum_psum.tile([P, GROUP_COLS], F32, name="sums", tag="sums")
+            woven = lag == MULTIPLY_LAG and step != tanh_step
+            for e in range(PAIR):
+                for b in range(BANKS_PER_ROW * e, BANKS_PER_ROW * (e + 1)):
+                    transpose_bank(step, b)
+                if woven:
+                    for index in due:
+                        multiply_row(index, e)
+            if not woven:
+                for index in due:
+                    for e in range(PAIR):
+                        multiply_row(index, e)
             grouped[step] = grouped_pool.tile(
                 [P, PAIR * CHANNELS], BF16, name="grouped", tag="grouped", align_bytes=64
             )
@@ -512,6 +517,7 @@ def tile_mamba2backbone_pb_kernel(
             for b in range(BANKS_PER_GROUP):
                 empty_group_bank(step, b, b < on_vector)
                 if b == 1:
+                    when_due(step, "dt", SUMS_LAG, dt_sigmoid)
                     if step >= tanh_step and decays_done < min(softplus_done, GROUPS):
                         decay_exp(decays_done)
                         decays_done += 1
@@ -557,8 +563,6 @@ def tile_mamba2backbone_pb_kernel(
             if step == last_group:
                 gate_the_change(GROUPS - 3)
             when_due(step, "z", SUMS_LAG, add_deter)
-
-            when_due(step, "dt", SUMS_LAG, dt_sigmoid)
 
         j = GROUPS - 1
         last_pair = pairs - 1

@@ -28,6 +28,7 @@ GROUP_WORDS = PAIR * PASSES * P
 
 GATES = ["dt", "b", "c", "z"]
 MULTIPLY_LAG = 2
+DT_SUMS_LAG = 2
 SUMS_LAG = MULTIPLY_LAG + 1
 FLIP_BANKS = 5
 SUM_BANKS = 3
@@ -468,7 +469,7 @@ def tile_mamba2backbone_pb_kernel(
 
         n_groups = len(GATES) * GROUPS
         last_group = n_groups - 1
-        log_step = GROUPS + SUMS_LAG
+        log_step = GROUPS + DT_SUMS_LAG
         logs_in_step = {log_step: 3, log_step + 1: 5}
         tanh_step = log_step + len(logs_in_step)
         vector_banks = {log_step: 4, log_step + 1: 4, tanh_step: 2}
@@ -481,16 +482,16 @@ def tile_mamba2backbone_pb_kernel(
             if step >= 2:
                 quantise_group(step - 1)
 
-            when_due(step, "dt", SUMS_LAG, dt_argument)
+            when_due(step, "dt", DT_SUMS_LAG, dt_argument)
             if step >= tanh_step:
-                while b_done < GROUPS and b_done + GROUPS + SUMS_LAG <= step:
+                while b_done < GROUPS and b_done + GROUPS < multiplied:
                     b_tanh(b_done)
                     b_done += 1
             when_due(step, "z", SUMS_LAG, z_tanh)
             if step == last_group:
                 z_tanh(GROUPS - 3)
 
-            lag = MULTIPLY_LAG if 4 <= step < last_group - 1 else 1
+            lag = MULTIPLY_LAG if GROUPS < step < last_group - 1 else 1
             due = range(multiplied, step - lag + 1)
             multiplied = max(multiplied, step - lag + 1)
             for index in due:
@@ -517,7 +518,7 @@ def tile_mamba2backbone_pb_kernel(
             for b in range(BANKS_PER_GROUP):
                 empty_group_bank(step, b, b < on_vector)
                 if b == 1:
-                    when_due(step, "dt", SUMS_LAG, dt_sigmoid)
+                    when_due(step, "dt", DT_SUMS_LAG, dt_sigmoid)
                     if step >= tanh_step and decays_done < min(softplus_done, GROUPS):
                         decay_exp(decays_done)
                         decays_done += 1
@@ -539,7 +540,7 @@ def tile_mamba2backbone_pb_kernel(
                 deter_by_k = transpose_tokens(deter_rows, "deter")
             if step + LOADS_AHEAD < n_groups:
                 load_group(step + LOADS_AHEAD)
-            if step == GROUPS:
+            if step == n_groups - LOADS_AHEAD:
                 nc.sync.dma_start(out=norm_gain[:], in_=norm_w.partition_broadcast(P))
 
             when_due(step, "c", SUMS_LAG, c_times_state)
@@ -559,7 +560,7 @@ def tile_mamba2backbone_pb_kernel(
                         softplus_done += 1
             when_due(step, "dt", SUMS_LAG + 1, skip_minus_deter)
             when_due(step, "z", SUMS_LAG, gate_the_change)
-            when_due(step, "z", -1, y_minus_deter)
+            when_due(step, "z", 0, y_minus_deter)
             if step == last_group:
                 gate_the_change(GROUPS - 3)
             when_due(step, "z", SUMS_LAG, add_deter)

@@ -124,18 +124,34 @@ def tile_mamba2backbone_pb_kernel(
             else:
                 nc.scalar.copy(out=out_words, in_=bank_view)
 
-        def transpose_tokens(rows, name):
+        def order_words(rows, g):
+            words = rows[:].bitcast(F32).rearrange("p (t w) -> p t w", t=TOKENS // P)
+            ordered = keep.tile([P, TOKENS // P * PAIR * P], F32, name="ordered%d" % g)
+            nc.vector.tensor_copy(
+                out=ordered[:].rearrange("p (t u q) -> p t u q", u=PAIR, q=P),
+                in_=words[:, :, PAIR * P * g : PAIR * P * (g + 1)].rearrange(
+                    "p t (q u) -> p t u q", u=PAIR
+                ),
+            )
+            return ordered
+
+        def transpose_tokens(rows, name, order_first):
             words = rows[:].bitcast(F32)
             tiles = []
+            if order_first:
+                ordered = [order_words(rows, g) for g in range(PASSES)]
             for g in range(PASSES):
                 bank = flip_psum.tile([P, BANK], F32, tag="flip")
                 for u in range(PAIR):
                     for t in range(TOKENS // P):
-                        first_word = ROW_WORDS * t + P * PAIR * g
+                        if order_first:
+                            first_word = P * (PAIR * t + u)
+                            source = ordered[g][:, first_word : first_word + P]
+                        else:
+                            first_word = ROW_WORDS * t + P * PAIR * g
+                            source = words[:, first_word + u : first_word + PAIR * P : PAIR]
                         nc.tensor.transpose(
-                            bank[:, TOKENS * u + P * t : TOKENS * u + P * (t + 1)],
-                            words[:, first_word + u : first_word + PAIR * P : PAIR],
-                            ident[:],
+                            bank[:, TOKENS * u + P * t : TOKENS * u + P * (t + 1)], source, ident[:]
                         )
                 by_k = keep.tile([P, TOKENS * PACK], BF16, name="%s%d" % (name, g), align_bytes=64)
                 empty_bank(
@@ -193,16 +209,34 @@ def tile_mamba2backbone_pb_kernel(
         def scalar_of(columns, j, e):
             return columns[:, PAIR * j + e : PAIR * j + e + 1]
 
-        def group_tiles(name):
-            return [keep.tile([P, GROUP_COLS], F32, name="%s%d" % (name, j)) for j in range(GROUPS)]
+        def pair_tiles(name):
+            return [
+                keep.tile([P, PAIR * GROUP_COLS], F32, name="%s%d" % (name, g)) for g in range(PASSES)
+            ]
+
+        def by_group(tiles):
+            return [
+                tiles[j // PAIR][:, GROUP_COLS * (j % PAIR) : GROUP_COLS * (j % PAIR + 1)]
+                for j in range(GROUPS)
+            ]
+
+        def quarters(pair_tile):
+            return pair_tile[:].rearrange("p (c t) -> p c t", c=PACK)
+
+        def pair_view(tiles, g):
+            return tiles[g][:].rearrange("p (t c) -> p c t", c=PACK)
 
         def halves(group_tile):
             return group_tile[:].rearrange("p (e t) -> p e t", e=PAIR)
 
-        soft = group_tiles("soft")
-        decay = group_tiles("decay")
-        state = group_tiles("state")
-        mix = group_tiles("mix")
+        soft_pairs = pair_tiles("soft")
+        decay_pairs = pair_tiles("decay")
+        state_pairs = pair_tiles("state")
+        mix_pairs = pair_tiles("mix")
+
+        b_gate_pairs = pair_tiles("b")
+        soft, decay, state = by_group(soft_pairs), by_group(decay_pairs), by_group(state_pairs)
+        mix, b_gate = by_group(mix_pairs), by_group(b_gate_pairs)
 
         banks = {}
         grouped = {}
@@ -285,9 +319,12 @@ def tile_mamba2backbone_pb_kernel(
         def dt_log(j):
             nc.scalar.activation(out=decay[j][:], in_=decay[j][:], func=ACT.Ln)
 
-        def dt_softplus(j):
+        def dt_softplus(g):
             nc.vector.tensor_tensor(
-                out=soft[j][:], in0=soft[j][:], in1=decay[j][:], op=ALU.subtract
+                out=soft_pairs[g][:],
+                in0=soft_pairs[g][:],
+                in1=decay_pairs[g][:],
+                op=ALU.subtract,
             )
 
         def skip_minus_deter(j):
@@ -301,12 +338,12 @@ def tile_mamba2backbone_pb_kernel(
                     op1=ALU.subtract,
                 )
 
-        def dt_times_x(j):
+        def dt_times_x(g):
             nc.vector.scalar_tensor_tensor(
-                out=halves(state[j]),
-                in0=halves(soft[j]),
+                out=quarters(state_pairs[g]),
+                in0=quarters(soft_pairs[g]),
                 scalar=DT_MIN - FLOOR,
-                in1=group_view(x_by_k, j),
+                in1=pair_view(x_by_k, g),
                 op0=ALU.add,
                 op1=ALU.mult,
             )
@@ -322,24 +359,26 @@ def tile_mamba2backbone_pb_kernel(
                     scale=scalar_of(a_neg, j, e),
                 )
 
-        def decay_times_deter(j):
+        def decay_times_deter(g):
             nc.vector.tensor_tensor(
-                out=halves(decay[j]),
-                in0=halves(decay[j]),
-                in1=group_view(deter_by_k, j),
+                out=quarters(decay_pairs[g]),
+                in0=quarters(decay_pairs[g]),
+                in1=pair_view(deter_by_k, g),
                 op=ALU.mult,
             )
-
-        b_gate = group_tiles("b")
 
         def b_tanh(j):
             activate_sums("b", j, b_gate[j], ACT.Tanh, rows_of(B_B), 1.0)
 
-        def input_term(j):
-            nc.vector.tensor_tensor(out=state[j][:], in0=state[j][:], in1=b_gate[j][:], op=ALU.mult)
+        def input_term(g):
+            nc.vector.tensor_tensor(
+                out=state_pairs[g][:], in0=state_pairs[g][:], in1=b_gate_pairs[g][:], op=ALU.mult
+            )
 
-        def new_state(j):
-            nc.vector.tensor_tensor(out=state[j][:], in0=state[j][:], in1=decay[j][:], op=ALU.add)
+        def new_state(g):
+            nc.vector.tensor_tensor(
+                out=state_pairs[g][:], in0=state_pairs[g][:], in1=decay_pairs[g][:], op=ALU.add
+            )
 
         def c_times_state(j):
             for e in range(PAIR):
@@ -456,26 +495,28 @@ def tile_mamba2backbone_pb_kernel(
                 stage(j)
 
         chain = []
-        for k in range(GROUPS + 3):
-            for stage, j in [
+        for k in range(PASSES + 1):
+            for stage, g in [
                 (dt_softplus, k),
-                (new_state, k - 3),
-                (input_term, k - 2),
-                (decay_times_deter, k - 2),
-                (dt_times_x, k - 1),
+                (input_term, k - 1),
+                (decay_times_deter, k - 1),
+                (dt_times_x, k),
+                (new_state, k - 1),
             ]:
-                if 0 <= j < GROUPS:
-                    chain.append((stage, j))
+                if 0 <= g < PASSES:
+                    chain.append((stage, g))
 
         n_groups = len(GATES) * GROUPS
         last_group = n_groups - 1
         log_step = GROUPS + DT_SUMS_LAG
         logs_in_step = {log_step: 3, log_step + 1: 5}
         tanh_step = log_step + len(logs_in_step)
-        vector_banks = {log_step: 4, log_step + 1: 4, tanh_step: 2}
+        vector_banks = {log_step: 4, log_step + 1: 3, tanh_step: 2}
         logs_done = 0
         decays_done = 0
         softplus_done = 0
+        states_done = 0
+        slots = 0
         b_done = 0
         multiplied = 0
         for step in range(n_groups):
@@ -512,14 +553,14 @@ def tile_mamba2backbone_pb_kernel(
             )
 
             if step < GROUPS:
-                on_vector = 1
+                on_vector = 2
             else:
                 on_vector = vector_banks.get(step, 0)
             for b in range(BANKS_PER_GROUP):
                 empty_group_bank(step, b, b < on_vector)
                 if b == 1:
                     when_due(step, "dt", DT_SUMS_LAG, dt_sigmoid)
-                    if step >= tanh_step and decays_done < min(softplus_done, GROUPS):
+                    if step >= tanh_step and decays_done < softplus_done:
                         decay_exp(decays_done)
                         decays_done += 1
                     if step in logs_in_step:
@@ -531,19 +572,20 @@ def tile_mamba2backbone_pb_kernel(
 
             if step == 0:
                 quantise_group(0)
-                x_by_k = transpose_tokens(x_rows, "x")
+                x_by_k = transpose_tokens(x_rows, "x", False)
                 quantise_x()
             if step == 1:
                 transpose_vectors()
                 nc.scalar.activation(out=a_log[:], in_=a_held[:], func=ACT.Sigmoid)
             if step == 3:
-                deter_by_k = transpose_tokens(deter_rows, "deter")
+                deter_by_k = transpose_tokens(deter_rows, "deter", True)
             if step + LOADS_AHEAD < n_groups:
                 load_group(step + LOADS_AHEAD)
             if step == n_groups - LOADS_AHEAD:
                 nc.sync.dma_start(out=norm_gain[:], in_=norm_w.partition_broadcast(P))
 
             when_due(step, "c", SUMS_LAG, c_times_state)
+            assert min(step - SUMS_LAG - 2 * GROUPS, GROUPS - 1) < states_done
             if step == log_step + 1:
                 nc.vector.tensor_tensor(
                     out=a_neg[:], in0=a_log[:], in1=a_held[:], op=ALU.subtract
@@ -552,12 +594,19 @@ def tile_mamba2backbone_pb_kernel(
                     out=a_shift[:], in0=a_neg[:], scalar1=DT_MIN - FLOOR
                 )
             if step > log_step:
-                slots = (4 if step < 2 * GROUPS else 3) - on_vector
-                due, chain = chain[:slots], chain[slots:]
-                for stage, j in due:
-                    stage(j)
+                slots += (4 if step < 2 * GROUPS else 3) - on_vector
+                due, chain = chain[: slots // PAIR], chain[slots // PAIR :]
+                slots %= PAIR
+                for stage, g in due:
+                    stage(g)
                     if stage == dt_softplus:
-                        softplus_done += 1
+                        softplus_done += PAIR
+                    if stage == decay_times_deter:
+                        assert decays_done >= PAIR * (g + 1)
+                    if stage == input_term:
+                        assert b_done >= PAIR * (g + 1)
+                    if stage == new_state:
+                        states_done += PAIR
             when_due(step, "dt", SUMS_LAG + 1, skip_minus_deter)
             when_due(step, "z", SUMS_LAG, gate_the_change)
             when_due(step, "z", 0, y_minus_deter)

@@ -58,6 +58,7 @@ def tile_mamba2backbone_pb_kernel(
         const = stack.enter_context(tc.tile_pool(name="const", bufs=1))
         keep = stack.enter_context(tc.tile_pool(name="keep", bufs=1))
         raw_pool = stack.enter_context(tc.tile_pool(name="raw", bufs=LOADS_AHEAD + 2))
+        ordered_pool = stack.enter_context(tc.tile_pool(name="ordered", bufs=2))
         grouped_pool = stack.enter_context(tc.tile_pool(name="grouped", bufs=3))
         mx_pool = stack.enter_context(tc.tile_pool(name="mx", bufs=3))
         temp = stack.enter_context(tc.tile_pool(name="temp", bufs=3))
@@ -82,6 +83,7 @@ def tile_mamba2backbone_pb_kernel(
             return rows
 
         raw = {}
+        raw_tiles = {}
 
         norm_gain = const.tile([P, CHANNELS], BF16)
 
@@ -94,6 +96,7 @@ def tile_mamba2backbone_pb_kernel(
 
         def load_group(index):
             rows = load_rows(group_rows(index))
+            raw_tiles[index] = rows
             raw[index] = [
                 rows[:, PAIR * BANK * b : PAIR * BANK * (b + 1)] for b in range(BANKS_PER_GROUP)
             ]
@@ -124,29 +127,30 @@ def tile_mamba2backbone_pb_kernel(
             else:
                 nc.scalar.copy(out=out_words, in_=bank_view)
 
-        def order_words(rows, g):
-            words = rows[:].bitcast(F32).rearrange("p (t w) -> p t w", t=TOKENS // P)
-            ordered = keep.tile([P, TOKENS // P * PAIR * P], F32, name="ordered%d" % g)
-            nc.vector.tensor_copy(
-                out=ordered[:].rearrange("p (t u q) -> p t u q", u=PAIR, q=P),
-                in_=words[:, :, PAIR * P * g : PAIR * P * (g + 1)].rearrange(
-                    "p t (q u) -> p t u q", u=PAIR
-                ),
-            )
-            return ordered
+        def order_words(on_vector, ordered, words):
+            in_words = words.rearrange("p t (w u) -> p t u w", u=PAIR)
+            out_words = ordered.rearrange("p t (u w) -> p t u w", u=PAIR)
+            if on_vector:
+                nc.vector.tensor_copy(out=out_words, in_=in_words)
+            else:
+                nc.scalar.copy(out=out_words, in_=in_words)
 
         def transpose_tokens(rows, name, order_first):
             words = rows[:].bitcast(F32)
             tiles = []
             if order_first:
-                ordered = [order_words(rows, g) for g in range(PASSES)]
+                by_tile = words.rearrange("p (t w) -> p t w", t=TOKENS // P)
+                ordered = keep.tile([P, PASSES, TOKENS // P, PAIR * P], F32, name=name + "_ordered")
+                for g in range(PASSES):
+                    order_words(
+                        True, ordered[:, g, :, :], by_tile[:, :, PAIR * P * g : PAIR * P * (g + 1)]
+                    )
             for g in range(PASSES):
                 bank = flip_psum.tile([P, BANK], F32, tag="flip")
                 for u in range(PAIR):
                     for t in range(TOKENS // P):
                         if order_first:
-                            first_word = P * (PAIR * t + u)
-                            source = ordered[g][:, first_word : first_word + P]
+                            source = ordered[:, g, t, P * u : P * (u + 1)]
                         else:
                             first_word = ROW_WORDS * t + P * PAIR * g
                             source = words[:, first_word + u : first_word + PAIR * P : PAIR]
@@ -238,6 +242,15 @@ def tile_mamba2backbone_pb_kernel(
         soft, decay, state = by_group(soft_pairs), by_group(decay_pairs), by_group(state_pairs)
         mix, b_gate = by_group(mix_pairs), by_group(b_gate_pairs)
 
+        ordered_rows = {}
+
+        def order_row(index, e, on_vector):
+            ordered_rows[index, e] = ordered_pool.tile(
+                [P, 1, ROW_WORDS], F32, name="ordered", tag="ordered"
+            )
+            words = raw_tiles[index][:].bitcast(F32).rearrange("p (e w) -> p e w", e=PAIR)
+            order_words(on_vector, ordered_rows[index, e][:], words[:, e : e + 1, :])
+
         banks = {}
         grouped = {}
         codes = {}
@@ -245,16 +258,18 @@ def tile_mamba2backbone_pb_kernel(
         sums = {}
 
         def transpose_bank(index, b):
-            words = raw[index][b].bitcast(F32)
+            e, half = b // BANKS_PER_ROW, b % BANKS_PER_ROW
             bank = flip_psum.tile([P, BANK], F32, tag="flip")
             for piece in range(BANK // P):
-                first_word = P * PAIR * (piece // PAIR)
-                u = piece % PAIR
-                nc.tensor.transpose(
-                    bank[:, P * piece : P * (piece + 1)],
-                    words[:, first_word + u : first_word + PAIR * P : PAIR],
-                    ident[:],
-                )
+                g, u = piece // PAIR, piece % PAIR
+                if (index, e) in ordered_rows:
+                    first_word = BANK * u + P * (PAIR * half + g)
+                    words = ordered_rows[index, e][:, 0, first_word : first_word + P]
+                else:
+                    first_word = P * PAIR * g + u
+                    last_word = P * PAIR * (g + 1)
+                    words = raw[index][b].bitcast(F32)[:, first_word:last_word:PAIR]
+                nc.tensor.transpose(bank[:, P * piece : P * (piece + 1)], words, ident[:])
             banks[index, b] = bank
 
         def empty_group_bank(index, b, on_vector):
@@ -552,7 +567,7 @@ def tile_mamba2backbone_pb_kernel(
                 [P, PAIR * CHANNELS], BF16, name="grouped", tag="grouped", align_bytes=64
             )
 
-            if step < GROUPS:
+            if step < log_step:
                 on_vector = 2
             else:
                 on_vector = vector_banks.get(step, 0)
@@ -560,6 +575,8 @@ def tile_mamba2backbone_pb_kernel(
                 empty_group_bank(step, b, b < on_vector)
                 if b == 1:
                     when_due(step, "dt", DT_SUMS_LAG, dt_sigmoid)
+                    if step + 1 in (3 * GROUPS, 3 * GROUPS + 2):
+                        order_row(step + 1, 1, False)
                     if step >= tanh_step and decays_done < softplus_done:
                         decay_exp(decays_done)
                         decays_done += 1
@@ -608,6 +625,8 @@ def tile_mamba2backbone_pb_kernel(
                     if stage == new_state:
                         states_done += PAIR
             when_due(step, "dt", SUMS_LAG + 1, skip_minus_deter)
+            if step + 1 < log_step and (step + 1) % 3 == 0:
+                order_row(step + 1, 1, True)
             when_due(step, "z", SUMS_LAG, gate_the_change)
             when_due(step, "z", 0, y_minus_deter)
             if step == last_group:

@@ -625,8 +625,6 @@ def tile_mamba2backbone_pb_kernel(
                     if stage == new_state:
                         states_done += PAIR
             when_due(step, "dt", SUMS_LAG + 1, skip_minus_deter)
-            if step + 1 < log_step and (step + 1) % 3 == 0:
-                order_row(step + 1, 1, True)
             when_due(step, "z", SUMS_LAG, gate_the_change)
             when_due(step, "z", 0, y_minus_deter)
             if step == last_group:
@@ -639,35 +637,40 @@ def tile_mamba2backbone_pb_kernel(
         new_codes(last_group)
         sums[last_group] = sum_psum.tile([P, GROUP_COLS], F32, name="sums", tag="sums")
         half_words = GROUP_WORDS // PAIR
+        first, second = tiles
         quantise_columns(last_group, 0, half_words)
-        add_deter(j - 2)
+        add_deter(j - 2, first)
         quantise_columns(last_group, half_words, GROUP_WORDS)
         flip_back(0, 0)
         flip_back(1, 0)
         for tokens in tiles:
             for e in range(PAIR):
                 multiply_row(last_group, e, tokens)
-        z_tanh(j - 1)
-        gate_the_change(j - 1)
-        add_deter(j - 1)
+        flip_back(2, 0)
+        for tokens in tiles:
+            z_tanh(j - 1, tokens)
         add_squares(0, 0)
-        z_tanh(j, tiles[0])
-        gate_the_change(j, tiles[0])
-        add_deter(j, tiles[0])
+        z_tanh(j, first)
         add_squares(1, 0)
-        z_tanh(j, tiles[1])
-        gate_the_change(j, tiles[1])
-        add_deter(j, tiles[1])
-        for pair, t in [(2, 0), (0, 1), (1, 1), (last_pair, 0), (2, 1), (last_pair, 1)]:
-            flip_back(pair, t)
-        for pair, t in [(2, 0), (0, 1), (last_pair, 0)]:
-            add_squares(pair, t)
+        z_tanh(j, second)
+        add_squares(2, 0)
+        for jj in (j - 1, j):
+            gate_the_change(jj, first)
+            add_deter(jj, first)
+        flip_back(last_pair, 0)
+        add_squares(last_pair, 0)
+        add_deter(j - 2, second)
+        for jj in (j - 1, j):
+            gate_the_change(jj, second)
+            add_deter(jj, second)
+        for pair in range(pairs):
+            flip_back(pair, 1)
         finish_norm(0)
-        for pair in range(1, pairs):
+        for pair in range(pairs):
             add_squares(pair, 1)
         for pair in range(pairs):
             store(pair, 0)
-            if pair == 1:
+            if pair == 2:
                 finish_norm(1)
         for pair in range(pairs):
             store(pair, 1)

@@ -552,17 +552,11 @@ def tile_mamba2backbone_pb_kernel(
             multiplied = max(multiplied, step - lag + 1)
             for index in due:
                 sums[index] = sum_psum.tile([P, GROUP_COLS], F32, name="sums", tag="sums")
-            woven = lag == MULTIPLY_LAG and step != tanh_step
-            for e in range(PAIR):
-                for b in range(BANKS_PER_ROW * e, BANKS_PER_ROW * (e + 1)):
-                    transpose_bank(step, b)
-                if woven:
-                    for index in due:
-                        multiply_row(index, e)
-            if not woven:
-                for index in due:
-                    for e in range(PAIR):
-                        multiply_row(index, e)
+            for b in range(BANKS_PER_GROUP):
+                transpose_bank(step, b)
+            for index in due:
+                for e in range(PAIR):
+                    multiply_row(index, e)
             grouped[step] = grouped_pool.tile(
                 [P, PAIR * CHANNELS], BF16, name="grouped", tag="grouped", align_bytes=64
             )
@@ -625,6 +619,8 @@ def tile_mamba2backbone_pb_kernel(
                     if stage == new_state:
                         states_done += PAIR
             when_due(step, "dt", SUMS_LAG + 1, skip_minus_deter)
+            if step + 1 < log_step and (step + 1) % 3 == 0:
+                order_row(step + 1, 1, True)
             when_due(step, "z", SUMS_LAG, gate_the_change)
             when_due(step, "z", 0, y_minus_deter)
             if step == last_group:
@@ -654,15 +650,17 @@ def tile_mamba2backbone_pb_kernel(
         add_squares(1, 0)
         z_tanh(j, second)
         add_squares(2, 0)
-        for jj in (j - 1, j):
-            gate_the_change(jj, first)
-            add_deter(jj, first)
+        gate_the_change(j - 1, first)
+        add_deter(j - 2, second)
+        add_deter(j - 1, first)
+        gate_the_change(j, first)
+        gate_the_change(j - 1, second)
+        add_deter(j, first)
         flip_back(last_pair, 0)
         add_squares(last_pair, 0)
-        add_deter(j - 2, second)
-        for jj in (j - 1, j):
-            gate_the_change(jj, second)
-            add_deter(jj, second)
+        gate_the_change(j, second)
+        add_deter(j - 1, second)
+        add_deter(j, second)
         for pair in range(pairs):
             flip_back(pair, 1)
         finish_norm(0)

from contextlib import ExitStack

import concourse.mybir as mybir
from concourse.masks import make_identity

F32 = mybir.dt.float32
BF16 = mybir.dt.bfloat16
U32 = mybir.dt.uint32
U8 = mybir.dt.uint8
FP8X4 = mybir.dt.float8_e4m3fn_x4
ACT = mybir.ActivationFunctionType
ALU = mybir.AluOpType

P = 128
TOKENS = 256
CHANNELS = 2048
PAIR = 2
PACK = 4
PASSES = CHANNELS // (P * PACK)
GROUP_ROWS = PAIR * P
GROUPS = CHANNELS // GROUP_ROWS
GROUP_COLS = PAIR * TOKENS
ROW_WORDS = CHANNELS // PAIR
BANK = 512
BANKS_PER_ROW = ROW_WORDS // BANK
BANKS_PER_GROUP = PAIR * BANKS_PER_ROW
GROUP_WORDS = PAIR * PASSES * P

GATES = ["dt", "b", "c", "z"]
MULTIPLY_LAG = 2
DT_SUMS_LAG = 2
SUMS_LAG = MULTIPLY_LAG + 1
FLIP_BANKS = 5
SUM_BANKS = 3
LOADS_AHEAD = 4
EPS = 1e-4
DT_MIN = 1e-4
FLOOR = 20.0

A_BASE = 0
DT_B = 1
B_B = 2
C_B = 3
Z_B = 4
SKIP = 5

FLOPS = 4 * 2 * TOKENS * CHANNELS * CHANNELS


def tile_mamba2backbone_pb_kernel(
    tc, x, deter, a_base, dt_w, dt_b, b_w, b_b, c_w, c_b, z_w, z_b, skip, norm_w, out
):
    nc = tc.nc
    weights = {"dt": dt_w, "c": c_w, "b": b_w, "z": z_w}
    vectors = [a_base, dt_b, b_b, c_b, z_b, skip]

    with ExitStack() as stack:
        const = stack.enter_context(tc.tile_pool(name="const", bufs=1))
        keep = stack.enter_context(tc.tile_pool(name="keep", bufs=1))
        raw_pool = stack.enter_context(tc.tile_pool(name="raw", bufs=LOADS_AHEAD + 2))
        ordered_pool = stack.enter_context(tc.tile_pool(name="ordered", bufs=2))
        grouped_pool = stack.enter_context(tc.tile_pool(name="grouped", bufs=3))
        mx_pool = stack.enter_context(tc.tile_pool(name="mx", bufs=3))
        temp = stack.enter_context(tc.tile_pool(name="temp", bufs=3))
        flip_psum = stack.enter_context(tc.psum_pool(name="flip", bufs=FLIP_BANKS))
        sum_psum = stack.enter_context(tc.psum_pool(name="sums", bufs=SUM_BANKS))
        stack.enter_context(tc.manual_schedule())

        ident = const.tile([P, P], F32)
        make_identity(nc, ident[:])
        one_col = const.tile([P, 1], F32)
        nc.vector.memset(one_col[:], 1.0)
        floor_col = const.tile([P, 1], F32)
        nc.vector.memset(floor_col[:], -FLOOR)
        minus_half = const.tile([P, 1], F32)
        nc.vector.memset(minus_half[:], -0.5)
        table_warm = const.tile([P, 1], F32)
        nc.scalar.activation(out=table_warm[:], in_=one_col[:], func=ACT.Sigmoid)

        def load_rows(rows_view):
            rows = raw_pool.tile([P, PAIR * CHANNELS], BF16, tag="raw")
            nc.sync.dma_start(out=rows[:].rearrange("p (r k) -> p r k", r=PAIR), in_=rows_view)
            return rows

        raw = {}
        raw_tiles = {}

        norm_gain = const.tile([P, CHANNELS], BF16)

        def group_rows(index):
            gate, j = GATES[index // GROUPS], index % GROUPS
            g, u = j // PAIR, j % PAIR
            rows = weights[gate][P * PACK * g : P * PACK * (g + 1), :]
            rows = rows.rearrange("(p c) k -> p c k", c=PACK)
            return rows[:, PAIR * u : PAIR * (u + 1), :]

        def load_group(index):
            rows = load_rows(group_rows(index))
            raw_tiles[index] = rows
            raw[index] = [
                rows[:, PAIR * BANK * b : PAIR * BANK * (b + 1)] for b in range(BANKS_PER_GROUP)
            ]

        bank_values = PAIR * BANK
        raw[0] = []
        for e, first, last in [(0, 0, bank_values), (0, bank_values, CHANNELS), (1, 0, CHANNELS)]:
            first_rows = keep.tile([P, last - first], BF16, name="first%d_%d" % (e, first))
            nc.sync.dma_start(out=first_rows[:], in_=group_rows(0)[:, e, first:last])
            for start in range(0, last - first, bank_values):
                raw[0].append(first_rows[:, start : start + bank_values])
        x_rows = load_rows(x.rearrange("(t p) k -> p t k", p=P))
        load_group(1)
        vector_rows = const.tile([P, PACK * P], BF16)
        nc.vector.memset(vector_rows[:], 0.0)
        for i, vector in enumerate(vectors):
            nc.scalar.dma_start(
                out=vector_rows[PASSES * i : PASSES * (i + 1), :],
                in_=vector.rearrange("(g c) -> g c", g=PASSES),
            )
        load_group(2)
        load_group(3)
        deter_rows = load_rows(deter.rearrange("(t p) k -> p t k", p=P))

        def empty_bank(on_vector, out_words, bank_view):
            if on_vector:
                nc.vector.tensor_copy(out=out_words, in_=bank_view)
            else:
                nc.scalar.copy(out=out_words, in_=bank_view)

        def order_words(on_vector, ordered, words):
            in_words = words.rearrange("p t (w u) -> p t u w", u=PAIR)
            out_words = ordered.rearrange("p t (u w) -> p t u w", u=PAIR)
            if on_vector:
                nc.vector.tensor_copy(out=out_words, in_=in_words)
            else:
                nc.scalar.copy(out=out_words, in_=in_words)

        def transpose_tokens(rows, name, order_first):
            words = rows[:].bitcast(F32)
            tiles = []
            if order_first:
                by_tile = words.rearrange("p (t w) -> p t w", t=TOKENS // P)
                ordered = keep.tile([P, PASSES, TOKENS // P, PAIR * P], F32, name=name + "_ordered")
                for g in range(PASSES):
                    order_words(
                        True, ordered[:, g, :, :], by_tile[:, :, PAIR * P * g : PAIR * P * (g + 1)]
                    )
            for g in range(PASSES):
                bank = flip_psum.tile([P, BANK], F32, tag="flip")
                for u in range(PAIR):
                    for t in range(TOKENS // P):
                        if order_first:
                            source = ordered[:, g, t, P * u : P * (u + 1)]
                        else:
                            first_word = ROW_WORDS * t + P * PAIR * g
                            source = words[:, first_word + u : first_word + PAIR * P : PAIR]
                        nc.tensor.transpose(
                            bank[:, TOKENS * u + P * t : TOKENS * u + P * (t + 1)], source, ident[:]
                        )
                by_k = keep.tile([P, TOKENS * PACK], BF16, name="%s%d" % (name, g), align_bytes=64)
                empty_bank(
                    g % 2 == 0,
                    by_k[:].bitcast(F32).rearrange("p (t u) -> p t u", u=PAIR),
                    bank[:].rearrange("p (u t) -> p t u", u=PAIR),
                )
                tiles.append(by_k)
            return tiles

        def group_view(tiles, j):
            g, u = j // PAIR, j % PAIR
            return tiles[g][:].rearrange("p (t c) -> p c t", c=PACK)[:, PAIR * u : PAIR * (u + 1), :]

        x_codes = keep.tile([P, PASSES * TOKENS], U32, align_bytes=64)
        x_scales = keep.tile([P, PASSES * TOKENS], U8, align_bytes=64)

        def quantise_x():
            for g in range(PASSES):
                cols = slice(TOKENS * g, TOKENS * (g + 1))
                nc.vector.quantize_mx(
                    out=x_codes[:, cols].bitcast(FP8X4), scales=x_scales[:, cols], in_=x_by_k[g][:]
                )

        vector_count = len(vectors)
        table = const.tile([P, PAIR * GROUPS * vector_count], F32)
        z_b_half = const.tile([P, PAIR * GROUPS], F32)
        dt_b_raised = const.tile([P, PAIR * GROUPS], F32)
        a_held = const.tile([P, PAIR * GROUPS], F32)
        a_log = const.tile([P, PAIR * GROUPS], F32)
        a_neg = const.tile([P, PAIR * GROUPS], F32)
        a_shift = const.tile([P, PAIR * GROUPS], F32)

        def transpose_vectors():
            vector_bank = flip_psum.tile([P, BANK], F32, tag="flip")
            words = vector_rows[:].bitcast(F32)
            for u in range(PAIR):
                nc.tensor.transpose(
                    vector_bank[:, P * u : P * (u + 1)], words[:, u : PAIR * P : PAIR], ident[:]
                )
                rows = PASSES * vector_count
                nc.vector.tensor_copy(
                    out=table[:].rearrange("p (r u e) -> p r u e", u=PAIR, e=PAIR)[:, :, u, :],
                    in_=vector_bank[:, P * u : P * u + rows]
                    .bitcast(BF16)
                    .rearrange("p (r e) -> p r e", e=PAIR),
                )
            nc.vector.tensor_scalar_mul(out=z_b_half[:], in0=rows_of(Z_B), scalar1=0.5)
            nc.vector.tensor_scalar_add(out=dt_b_raised[:], in0=rows_of(DT_B), scalar1=FLOOR)
            nc.vector.tensor_scalar_max(out=a_held[:], in0=rows_of(A_BASE), scalar1=-FLOOR)

        def rows_of(which):
            return table[:, PAIR * GROUPS * which : PAIR * GROUPS * (which + 1)]

        def scalar_of(columns, j, e):
            return columns[:, PAIR * j + e : PAIR * j + e + 1]

        def pair_tiles(name):
            return [
                keep.tile([P, PAIR * GROUP_COLS], F32, name="%s%d" % (name, g)) for g in range(PASSES)
            ]

        def by_group(tiles):
            return [
                tiles[j // PAIR][:, GROUP_COLS * (j % PAIR) : GROUP_COLS * (j % PAIR + 1)]
                for j in range(GROUPS)
            ]

        def quarters(pair_tile):
            return pair_tile[:].rearrange("p (c t) -> p c t", c=PACK)

        def pair_view(tiles, g):
            return tiles[g][:].rearrange("p (t c) -> p c t", c=PACK)

        def halves(group_tile):
            return group_tile[:].rearrange("p (e t) -> p e t", e=PAIR)

        soft_pairs = pair_tiles("soft")
        decay_pairs = pair_tiles("decay")
        state_pairs = pair_tiles("state")
        mix_pairs = pair_tiles("mix")

        b_gate_pairs = pair_tiles("b")
        soft, decay, state = by_group(soft_pairs), by_group(decay_pairs), by_group(state_pairs)
        mix, b_gate = by_group(mix_pairs), by_group(b_gate_pairs)

        ordered_rows = {}

        def order_row(index, e, on_vector):
            ordered_rows[index, e] = ordered_pool.tile(
                [P, 1, ROW_WORDS], F32, name="ordered", tag="ordered"
            )
            words = raw_tiles[index][:].bitcast(F32).rearrange("p (e w) -> p e w", e=PAIR)
            order_words(on_vector, ordered_rows[index, e][:], words[:, e : e + 1, :])

        banks = {}
        grouped = {}
        codes = {}
        scales = {}
        sums = {}

        def transpose_bank(index, b):
            e, half = b // BANKS_PER_ROW, b % BANKS_PER_ROW
            bank = flip_psum.tile([P, BANK], F32, tag="flip")
            for piece in range(BANK // P):
                g, u = piece // PAIR, piece % PAIR
                if (index, e) in ordered_rows:
                    first_word = BANK * u + P * (PAIR * half + g)
                    words = ordered_rows[index, e][:, 0, first_word : first_word + P]
                else:
                    first_word = P * PAIR * g + u
                    last_word = P * PAIR * (g + 1)
                    words = raw[index][b].bitcast(F32)[:, first_word:last_word:PAIR]
                nc.tensor.transpose(bank[:, P * piece : P * (piece + 1)], words, ident[:])
            banks[index, b] = bank

        def empty_group_bank(index, b, on_vector):
            empty_bank(
                on_vector,
                grouped[index][:]
                .bitcast(F32)[:, BANK * b : BANK * (b + 1)]
                .rearrange("p (g n u) -> p g n u", g=PAIR, u=PAIR),
                banks[index, b][:].rearrange("p (g u n) -> p g n u", g=PAIR, u=PAIR),
            )

        def quantise_columns(index, first, last):
            nc.vector.quantize_mx(
                out=codes[index][:, first:last].bitcast(FP8X4),
                scales=scales[index][:, first:last],
                in_=grouped[index][:, PACK * first : PACK * last],
            )

        def new_codes(index):
            codes[index] = mx_pool.tile([P, GROUP_WORDS], U32, name="codes", align_bytes=64)
            scales[index] = mx_pool.tile([P, GROUP_WORDS], U8, name="scales", align_bytes=64)

        def quantise_group(index):
            new_codes(index)
            quantise_columns(index, 0, GROUP_WORDS)

        ALL = slice(0, TOKENS)

        def multiply_row(index, e, tokens=ALL):
            for g in range(PASSES):
                w_cols = slice(P * (PASSES * e + g), P * (PASSES * e + g + 1))
                x_cols = slice(TOKENS * g + tokens.start, TOKENS * g + tokens.stop)
                nc.tensor.matmul_mx(
                    out=sums[index][:, TOKENS * e + tokens.start : TOKENS * e + tokens.stop],
                    lhsT=codes[index][:, w_cols].bitcast(FP8X4),
                    lhsT_scale=scales[index][:, w_cols],
                    rhs=x_codes[:, x_cols].bitcast(FP8X4),
                    rhs_scale=x_scales[:, x_cols],
                    start=(g == 0),
                    stop=(g == PASSES - 1),
                )

        def activate_sums(gate, j, out_tile, func, bias_columns, scale, tokens=ALL):
            for e in range(PAIR):
                cols = slice(TOKENS * e + tokens.start, TOKENS * e + tokens.stop)
                nc.scalar.activation(
                    out=out_tile[:, cols],
                    in_=sums[GROUPS * GATES.index(gate) + j][:, cols],
                    func=func,
                    bias=scalar_of(bias_columns, j, e),
                    scale=scale,
                )

        def dt_argument(j):
            activate_sums("dt", j, soft[j], ACT.Relu, dt_b_raised, 1.0)

        def dt_sigmoid(j):
            nc.scalar.activation(
                out=decay[j][:], in_=soft[j][:], func=ACT.Sigmoid, bias=floor_col[:]
            )

        def dt_log(j):
            nc.scalar.activation(out=decay[j][:], in_=decay[j][:], func=ACT.Ln)

        def dt_softplus(g):
            nc.vector.tensor_tensor(
                out=soft_pairs[g][:],
                in0=soft_pairs[g][:],
                in1=decay_pairs[g][:],
                op=ALU.subtract,
            )

        def skip_minus_deter(j):
            for e in range(PAIR):
                nc.vector.scalar_tensor_tensor(
                    out=halves(mix[j])[:, e, :],
                    in0=group_view(x_by_k, j)[:, e, :],
                    scalar=scalar_of(rows_of(SKIP), j, e),
                    in1=group_view(deter_by_k, j)[:, e, :],
                    op0=ALU.mult,
                    op1=ALU.subtract,
                )

        def dt_times_x(g):
            nc.vector.scalar_tensor_tensor(
                out=quarters(state_pairs[g]),
                in0=quarters(soft_pairs[g]),
                scalar=DT_MIN - FLOOR,
                in1=pair_view(x_by_k, g),
                op0=ALU.add,
                op1=ALU.mult,
            )

        def decay_exp(j):
            for e in range(PAIR):
                cols = slice(TOKENS * e, TOKENS * (e + 1))
                nc.scalar.activation(
                    out=decay[j][:, cols],
                    in_=soft[j][:, cols],
                    func=ACT.Exp,
                    bias=scalar_of(a_shift, j, e),
                    scale=scalar_of(a_neg, j, e),
                )

        def decay_times_deter(g):
            nc.vector.tensor_tensor(
                out=quarters(decay_pairs[g]),
                in0=quarters(decay_pairs[g]),
                in1=pair_view(deter_by_k, g),
                op=ALU.mult,
            )

        def b_tanh(j):
            activate_sums("b", j, b_gate[j], ACT.Tanh, rows_of(B_B), 1.0)

        def input_term(g):
            nc.vector.tensor_tensor(
                out=state_pairs[g][:], in0=state_pairs[g][:], in1=b_gate_pairs[g][:], op=ALU.mult
            )

        def new_state(g):
            nc.vector.tensor_tensor(
                out=state_pairs[g][:], in0=state_pairs[g][:], in1=decay_pairs[g][:], op=ALU.add
            )

        def c_times_state(j):
            for e in range(PAIR):
                cols = slice(TOKENS * e, TOKENS * (e + 1))
                nc.vector.scalar_tensor_tensor(
                    out=state[j][:, cols],
                    in0=sums[GROUPS * GATES.index("c") + j][:, cols],
                    scalar=scalar_of(rows_of(C_B), j, e),
                    in1=state[j][:, cols],
                    op0=ALU.add,
                    op1=ALU.mult,
                )

        def y_minus_deter(j):
            nc.vector.tensor_tensor(out=mix[j][:], in0=mix[j][:], in1=state[j][:], op=ALU.add)

        z_gate = {}

        def z_tanh(j, tokens=ALL):
            if j not in z_gate:
                z_gate[j] = temp.tile([P, GROUP_COLS], F32, name="z", tag="z")
            activate_sums("z", j, z_gate[j], ACT.Tanh, z_b_half, 0.5, tokens)

        def gate_the_change(j, tokens=ALL):
            nc.vector.scalar_tensor_tensor(
                out=halves(z_gate[j])[:, :, tokens],
                in0=halves(z_gate[j])[:, :, tokens],
                scalar=1.0,
                in1=halves(mix[j])[:, :, tokens],
                op0=ALU.add,
                op1=ALU.mult,
            )

        def add_deter(j, tokens=ALL):
            nc.vector.scalar_tensor_tensor(
                out=halves(mix[j])[:, :, tokens],
                in0=halves(z_gate[j])[:, :, tokens],
                scalar=0.5,
                in1=group_view(deter_by_k, j)[:, :, tokens],
                op0=ALU.mult,
                op1=ALU.add,
            )

        token_tiles = TOKENS // P
        groups_per_bank = BANK // GROUP_ROWS
        pairs = GROUPS // groups_per_bank
        parts = pairs + 1
        mean_square_parts = const.tile([P, token_tiles * parts], F32)
        nc.vector.memset(mean_square_parts[:], EPS)
        inv_rms = const.tile([P, token_tiles], F32)

        free_banks = FLIP_BANKS * [(flip_psum, "flip")] + SUM_BANKS * [(sum_psum, "sums")]
        out_banks = {}

        def flip_back(pair, t):
            pool, tag = free_banks[len(out_banks)]
            bank = pool.tile([P, BANK], F32, name="out_bank", tag=tag)
            for jj in range(groups_per_bank):
                for e in range(PAIR):
                    first = TOKENS * e + P * t
                    nc.tensor.transpose(
                        bank[:, P * (PAIR * jj + e) : P * (PAIR * jj + e + 1)],
                        mix[groups_per_bank * pair + jj][:, first : first + P],
                        ident[:],
                    )
            out_banks[pair, t] = bank

        def add_squares(pair, t):
            squares = temp.tile([P, BANK], F32, name="squares", tag="squares")
            column = parts * t + pair
            nc.scalar.activation(
                out=squares[:],
                in_=out_banks[pair, t][:],
                func=ACT.Square,
                scale=CHANNELS**-0.5,
                accum_out=mean_square_parts[:, column : column + 1],
            )

        def finish_norm(t):
            mean_square = const.tile([P, 1], F32, name="mean_square%d" % t)
            nc.vector.tensor_reduce(
                out=mean_square[:],
                in_=mean_square_parts[:, parts * t : parts * (t + 1)],
                axis=mybir.AxisListType.X,
                op=ALU.add,
            )
            nc.gpsimd.tensor_tensor(
                out=inv_rms[:, t : t + 1], in0=mean_square[:], in1=minus_half[:], op=ALU.pow
            )

        normed_rows = {}

        def store(pair, t):
            channels = slice(BANK * pair, BANK * (pair + 1))
            if pair == 0:
                normed_rows[t] = raw_pool.tile([P, PAIR * CHANNELS], BF16, name="normed", tag="raw")
            normed = normed_rows[t][:].bitcast(F32)[:, channels]
            by_channel = "p (c j e) -> p c j e"
            nc.vector.scalar_tensor_tensor(
                out=normed.rearrange(by_channel, j=groups_per_bank, e=PAIR),
                in0=out_banks[pair, t][:].rearrange(
                    "p (j e c) -> p c j e", j=groups_per_bank, e=PAIR
                ),
                scalar=inv_rms[:, t : t + 1],
                in1=norm_gain[:, channels].rearrange(by_channel, j=groups_per_bank, e=PAIR),
                op0=ALU.mult,
                op1=ALU.mult,
            )
            nc.sync.dma_start(out=out[P * t : P * (t + 1), channels], in_=normed)

        def when_due(step, gate, lag, stage):
            j = step - lag - GROUPS * GATES.index(gate)
            if 0 <= j < GROUPS:
                stage(j)

        chain = []
        for k in range(PASSES + 1):
            for stage, g in [
                (dt_softplus, k),
                (input_term, k - 1),
                (decay_times_deter, k - 1),
                (dt_times_x, k),
                (new_state, k - 1),
            ]:
                if 0 <= g < PASSES:
                    chain.append((stage, g))

        n_groups = len(GATES) * GROUPS
        last_group = n_groups - 1
        log_step = GROUPS + DT_SUMS_LAG
        logs_in_step = {log_step: 3, log_step + 1: 5}
        tanh_step = log_step + len(logs_in_step)
        vector_banks = {log_step: 4, log_step + 1: 3, tanh_step: 2}
        logs_done = 0
        decays_done = 0
        softplus_done = 0
        states_done = 0
        slots = 0
        b_done = 0
        multiplied = 0
        for step in range(n_groups):
            if step >= 2:
                quantise_group(step - 1)

            when_due(step, "dt", DT_SUMS_LAG, dt_argument)
            if step >= tanh_step:
                while b_done < GROUPS and b_done + GROUPS < multiplied:
                    b_tanh(b_done)
                    b_done += 1
            when_due(step, "z", SUMS_LAG, z_tanh)
            if step == last_group:
                z_tanh(GROUPS - 3)

            lag = MULTIPLY_LAG if GROUPS < step < last_group - 1 else 1
            due = range(multiplied, step - lag + 1)
            multiplied = max(multiplied, step - lag + 1)
            for index in due:
                sums[index] = sum_psum.tile([P, GROUP_COLS], F32, name="sums", tag="sums")
            for b in range(BANKS_PER_GROUP):
                transpose_bank(step, b)
            for index in due:
                for e in range(PAIR):
                    multiply_row(index, e)
            grouped[step] = grouped_pool.tile(
                [P, PAIR * CHANNELS], BF16, name="grouped", tag="grouped", align_bytes=64
            )

            if step < log_step:
                on_vector = 2
            else:
                on_vector = vector_banks.get(step, 0)
            for b in range(BANKS_PER_GROUP):
                empty_group_bank(step, b, b < on_vector)
                if b == 1:
                    when_due(step, "dt", DT_SUMS_LAG, dt_sigmoid)
                    if step + 1 in (3 * GROUPS, 3 * GROUPS + 2):
                        order_row(step + 1, 1, False)
                    if step >= tanh_step and decays_done < softplus_done:
                        decay_exp(decays_done)
                        decays_done += 1
                    if step in logs_in_step:
                        if logs_done == 0:
                            nc.scalar.activation(out=a_log[:], in_=a_log[:], func=ACT.Ln)
                        for j in range(logs_done, logs_done + logs_in_step[step]):
                            dt_log(j)
                        logs_done += logs_in_step[step]

            if step == 0:
                quantise_group(0)
                x_by_k = transpose_tokens(x_rows, "x", False)
                quantise_x()
            if step == 1:
                transpose_vectors()
                nc.scalar.activation(out=a_log[:], in_=a_held[:], func=ACT.Sigmoid)
            if step == 3:
                deter_by_k = transpose_tokens(deter_rows, "deter", True)
            if step + LOADS_AHEAD < n_groups:
                load_group(step + LOADS_AHEAD)
            if step == n_groups - LOADS_AHEAD:
                nc.sync.dma_start(out=norm_gain[:], in_=norm_w.partition_broadcast(P))

            when_due(step, "c", SUMS_LAG, c_times_state)
            assert min(step - SUMS_LAG - 2 * GROUPS, GROUPS - 1) < states_done
            if step == log_step + 1:
                nc.vector.tensor_tensor(
                    out=a_neg[:], in0=a_log[:], in1=a_held[:], op=ALU.subtract
                )
                nc.vector.tensor_scalar_mul(
                    out=a_shift[:], in0=a_neg[:], scalar1=DT_MIN - FLOOR
                )
            if step > log_step:
                slots += (4 if step < 2 * GROUPS else 3) - on_vector
                due, chain = chain[: slots // PAIR], chain[slots // PAIR :]
                slots %= PAIR
                for stage, g in due:
                    stage(g)
                    if stage == dt_softplus:
                        softplus_done += PAIR
                    if stage == decay_times_deter:
                        assert decays_done >= PAIR * (g + 1)
                    if stage == input_term:
                        assert b_done >= PAIR * (g + 1)
                    if stage == new_state:
                        states_done += PAIR
            when_due(step, "dt", SUMS_LAG + 1, skip_minus_deter)
            if step + 1 < log_step and (step + 1) % 3 == 0:
                order_row(step + 1, 1, True)
            when_due(step, "z", SUMS_LAG, gate_the_change)
            when_due(step, "z", 0, y_minus_deter)
            if step == last_group:
                gate_the_change(GROUPS - 3)
            when_due(step, "z", SUMS_LAG, add_deter)

        j = GROUPS - 1
        last_pair = pairs - 1
        tiles = [slice(P * t, P * (t + 1)) for t in range(token_tiles)]
        new_codes(last_group)
        sums[last_group] = sum_psum.tile([P, GROUP_COLS], F32, name="sums", tag="sums")
        half_words = GROUP_WORDS // PAIR
        first, second = tiles
        quantise_columns(last_group, 0, half_words)
        add_deter(j - 2, first)
        quantise_columns(last_group, half_words, GROUP_WORDS)
        flip_back(0, 0)
        flip_back(1, 0)
        for tokens in tiles:
            for e in range(PAIR):
                multiply_row(last_group, e, tokens)
        flip_back(2, 0)
        for tokens in tiles:
            z_tanh(j - 1, tokens)
        add_squares(0, 0)
        z_tanh(j, first)
        add_squares(1, 0)
        z_tanh(j, second)
        add_squares(2, 0)
        gate_the_change(j - 1, first)
        add_deter(j - 2, second)
        add_deter(j - 1, first)
        gate_the_change(j, first)
        gate_the_change(j - 1, second)
        add_deter(j, first)
        flip_back(last_pair, 0)
        add_squares(last_pair, 0)
        gate_the_change(j, second)
        add_deter(j - 1, second)
        add_deter(j, second)
        for pair in range(pairs):
            flip_back(pair, 1)
        finish_norm(0)
        for pair in range(pairs):
            add_squares(pair, 1)
        for pair in range(pairs):
            store(pair, 0)
            if pair == 2:
                finish_norm(1)
        for pair in range(pairs):
            store(pair, 1)
